import numpy as np
import ml_dtypes


def mxq(x, axis, fmt="e4m3"):
    dtype, down = {"e4m3": (ml_dtypes.float8_e4m3fn, 7), "e5m2": (ml_dtypes.float8_e5m2, 14)}[fmt]
    v = np.moveaxis(np.asarray(x, np.float32).astype(ml_dtypes.bfloat16).astype(np.float64), axis, -1)
    blocks = v.reshape(v.shape[:-1] + (-1, 32))
    amax = np.abs(blocks).max(-1, keepdims=True)
    byte = np.maximum(np.where(amax > 0, np.frexp(amax)[1] - 1 + 127, 0) - down, 1)
    scale = np.exp2(byte - 127.0)
    codes = (blocks / scale).astype(np.float32).astype(dtype).astype(np.float64)
    return np.moveaxis((codes * scale).reshape(v.shape), -1, axis)


WIDE = False


def mx_kscale(k):
    if not WIDE:
        return np.ones(k)
    levels = np.array([30, -30])
    if k % 512:
        return np.exp2(np.random.permutation(np.resize(levels, k // 32))).repeat(32)
    a = np.empty((k // 512, 16))
    for p in range(k // 512):
        a[p, :8] = np.random.permutation(np.resize(levels, 8))
        for g in range(8):
            far = levels[np.abs(levels - a[p, g]) >= 10]
            a[p, g + 8] = far[np.random.randint(len(far))]
    return np.exp2(a.ravel()).repeat(32)


BF16 = ml_dtypes.bfloat16


def bf(x):
    return np.asarray(x, np.float32).astype(BF16)


def f64(x):
    return np.asarray(x).astype(np.float64)


B, S, D, H, HD = 2, 256, 2048, 16, 128
E = H * HD
HP = HD // 2


def split_heads(t):
    return t.reshape(B, S, H, HD).transpose(0, 2, 1, 3)


def apply_rope(t, cos, sin):
    t1 = t[..., 0::2]
    t2 = t[..., 1::2]
    r1 = t1 * cos - t2 * sin
    r2 = t1 * sin + t2 * cos
    return np.stack([r1, r2], axis=-1).reshape(t.shape)


def setup_inputs():
    s = mx_kscale(D)
    ang = np.random.uniform(-np.pi, np.pi, (S, HP))
    return {"x": bf(np.random.standard_normal((B, S, D)) * s),
            "Wq": bf(np.random.standard_normal((D, E)) / np.sqrt(D) / s[:, None]),
            "Wk": bf(np.random.standard_normal((D, E)) / np.sqrt(D) / s[:, None]),
            "rope_cos": bf(np.cos(ang)),
            "rope_sin": bf(np.sin(ang))}


def reference(x, Wq, Wk, rope_cos, rope_sin):
    xq = mxq(f64(x), 2, "e5m2")
    q = split_heads(xq @ mxq(f64(Wq), 0, "e5m2"))
    k = split_heads(xq @ mxq(f64(Wk), 0, "e5m2"))
    cos, sin = f64(rope_cos), f64(rope_sin)
    return apply_rope(q, cos, sin), apply_rope(k, cos, sin)

@@ -1,0 +1,208 @@
+from contextlib import ExitStack
+
+import concourse.mybir as mybir
+from concourse.masks import make_identity
+
+F32 = mybir.dt.float32
+BF16 = mybir.dt.bfloat16
+U32 = mybir.dt.uint32
+U8 = mybir.dt.uint8
+FP8X4 = mybir.dt.float8_e5m2_x4
+MULT = mybir.AluOpType.mult
+ADD = mybir.AluOpType.add
+
+B, S, D, H, HD = 2, 256, 2048, 16, 128
+E = H * HD
+P = 128
+PASSES = D // 512
+CHUNK = 1024
+HALF = 512
+N_CHUNKS = 2 * E // CHUNK
+PE_COLS = (256, 128)
+SCALAR_COLS = (224, 320)
+RAW_BUFS = 8
+
+FLOPS = 2 * B * S * D * 2 * E
+
+
+def tile_llamaattention_pa_kernel(tc, x, Wq, Wk, rope_cos, rope_sin, out_0, out_1):
+    nc = tc.nc
+    weights = (Wq, Wk)
+    outs = (out_0, out_1)
+
+    with ExitStack() as ctx:
+        const = ctx.enter_context(tc.tile_pool(name="const", bufs=1))
+        xraw = ctx.enter_context(tc.tile_pool(name="xraw", bufs=2))
+        xgrp = ctx.enter_context(tc.tile_pool(name="xgrp", bufs=2))
+        wraw = ctx.enter_context(tc.tile_pool(name="wraw", bufs=RAW_BUFS))
+        wgrp = ctx.enter_context(tc.tile_pool(name="wgrp", bufs=4))
+        wcode = ctx.enter_context(tc.tile_pool(name="wcode", bufs=2))
+        ep = ctx.enter_context(tc.tile_pool(name="ep", bufs=4))
+        rp = ctx.enter_context(tc.tile_pool(name="rp", bufs=3))
+        accp = ctx.enter_context(tc.psum_pool(name="accp", bufs=6))
+        ptp = ctx.enter_context(tc.psum_pool(name="ptp", bufs=2))
+
+        raw_tiles = {}
+        x_tiles = {}
+
+        def w_rows(c, g, lo, hi):
+            w, j = c // 2, c % 2
+            return weights[w][512 * g : 512 * (g + 1), CHUNK * j + lo : CHUNK * j + hi].rearrange(
+                "(p t) c -> p t c", t=4
+            )
+
+        def new_raw(c, g):
+            raw = wraw.tile([P, 4, CHUNK], BF16, name="raw")
+            raw_tiles[(c, g)] = raw
+            return raw
+
+        def load_unit(c, g):
+            raw = new_raw(c, g)
+            nc.sync.dma_start(out=raw[:], in_=w_rows(c, g, 0, CHUNK))
+
+        def load_x(b):
+            x_sb = xraw.tile([P, 2, D], BF16, name="x_sb")
+            nc.sync.dma_start(out=x_sb[:], in_=x[b].rearrange("(p e) k -> p e k", e=2))
+            x_tiles[b] = x_sb
+
+        for g in range(PASSES):
+            raw = new_raw(0, g)
+            nc.sync.dma_start(out=raw[:, :, :HALF], in_=w_rows(0, g, 0, HALF))
+            if g < B:
+                load_x(g)
+        for g in range(PASSES):
+            nc.sync.dma_start(out=raw_tiles[(0, g)][:, :, HALF:], in_=w_rows(0, g, HALF, CHUNK))
+        for g in range(PASSES):
+            load_unit(1, g)
+
+        cos_sb = const.tile([P, 2, HD // 2], BF16, name="cos_sb")
+        sin_sb = const.tile([P, 2, HD // 2], BF16, name="sin_sb")
+        nc.scalar.dma_start(out=cos_sb[:], in_=rope_cos.rearrange("(p e) i -> p e i", e=2))
+        nc.scalar.dma_start(out=sin_sb[:], in_=rope_sin.rearrange("(p e) i -> p e i", e=2))
+        ident = const.tile([P, P], F32, name="ident")
+        make_identity(nc, ident[:])
+        ident_bf = const.tile([P, P], BF16, name="ident_bf")
+        make_identity(nc, ident_bf[:])
+        c2 = const.tile([P, 2, HD // 2, 2], F32, name="c2")
+        s2 = const.tile([P, 2, HD // 2, 2], F32, name="s2")
+        nc.gpsimd.tensor_copy(out=c2[:], in_=cos_sb[:].unsqueeze(3).to_broadcast([P, 2, HD // 2, 2]))
+        nc.gpsimd.tensor_copy(out=s2[:, :, :, 0:1], in_=sin_sb[:].unsqueeze(3))
+        nc.gpsimd.tensor_scalar(
+            out=s2[:, :, :, 1:2], in0=sin_sb[:].unsqueeze(3), scalar1=-1.0, scalar2=0.0, op0=MULT, op1=ADD
+        )
+        c4 = const.tile([P, 2, 4, HD], F32, name="c4")
+        s4 = const.tile([P, 2, 4, HD], F32, name="s4")
+        for e in range(2):
+            nc.gpsimd.tensor_copy(
+                out=c4[:, e, :, :],
+                in_=c2[:, e, :, :].rearrange("p i e -> p (i e)").unsqueeze(1).to_broadcast([P, 4, HD]),
+            )
+            nc.gpsimd.tensor_copy(
+                out=s4[:, e, :, :],
+                in_=s2[:, e, :, :].rearrange("p i e -> p (i e)").unsqueeze(1).to_broadcast([P, 4, HD]),
+            )
+
+        xc = const.tile([P, 2 * B, 512], U32, name="xc", align_bytes=64)
+        xs = const.tile([P, 2 * B, 512], U8, name="xs", align_bytes=64)
+
+        def prep_x(b, e):
+            m = 2 * b + e
+            words = x_tiles[b][:, e, :].bitcast(F32)
+            xg = xgrp.tile([P, D], BF16, name="xg", align_bytes=64)
+            xg_words = xg[:].bitcast(F32)
+            for gp in range(2):
+                bank = ptp.tile([P, 2, 2, P], F32, name="bank", tag="pt")
+                for gg in range(2):
+                    g = 2 * gp + gg
+                    for u in range(2):
+                        nc.tensor.transpose(bank[:, gg, u, :], words[:, 256 * g + u : 256 * (g + 1) : 2], ident[:])
+                nc.vector.tensor_copy(
+                    out=xg_words[:, 512 * gp : 512 * (gp + 1)].rearrange("p (g r u) -> p g r u", g=2, u=2),
+                    in_=bank[:].rearrange("p g u r -> p g r u"),
+                )
+            nc.vector.quantize_mx(out=xc[:, m, :].bitcast(FP8X4), scales=xs[:, m, :], in_=xg[:])
+
+        code_tiles = {}
+
+        def prep_w(c, n, g):
+            if (n, g) == (0, 0):
+                wc = wcode.tile([P, PASSES, CHUNK], U32, name="wc", align_bytes=64)
+                ws = wcode.tile([P, PASSES, CHUNK], U8, name="ws", align_bytes=64)
+                code_tiles[c] = (wc, ws)
+            wc, ws = code_tiles[c]
+            src = raw_tiles[(c, g)][:, :, HALF * n : HALF * (n + 1)]
+            grp = wgrp.tile([P, HALF, 4], BF16, name="grp", align_bytes=64)
+            pe_cols = PE_COLS[n]
+            s_end = pe_cols + SCALAR_COLS[n]
+            pt = ptp.tile([P, 256, 4], BF16, name="pt", tag="pt")
+            for c1 in range(0, pe_cols, P):
+                nc.tensor.matmul(
+                    out=pt[:, c1 : c1 + P, :],
+                    lhsT=ident_bf[:],
+                    rhs=src[:, :, c1 : c1 + P].rearrange("p t c -> p c t"),
+                    start=True,
+                    stop=True,
+                )
+            nc.scalar.copy(out=grp[:, :pe_cols, :], in_=pt[:, :pe_cols, :])
+            nc.scalar.copy(out=grp[:, pe_cols:s_end, :], in_=src[:, :, pe_cols:s_end].rearrange("p t c -> p c t"))
+            nc.vector.tensor_copy(out=grp[:, s_end:, :], in_=src[:, :, s_end:].rearrange("p t c -> p c t"))
+            cols = slice(HALF * n, HALF * (n + 1))
+            nc.vector.quantize_mx(
+                out=wc[:, g, cols].bitcast(FP8X4), scales=ws[:, g, cols], in_=grp[:].rearrange("p c t -> p (c t)")
+            )
+            if n == 1 and c + 2 < N_CHUNKS:
+                load_unit(c + 2, g)
+
+        r_tiles = {}
+
+        def bank_work(c, n, b, e):
+            wc, ws = code_tiles[c]
+            m = 2 * b + e
+            cols = slice(HALF * n, HALF * (n + 1))
+            acc = accp.tile([P, 512], F32, name="acc")
+            for g in range(PASSES):
+                nc.tensor.matmul_mx(
+                    out=acc[:],
+                    lhsT=xc[:, m, P * g : P * (g + 1)].bitcast(FP8X4),
+                    lhsT_scale=xs[:, m, P * g : P * (g + 1)],
+                    rhs=wc[:, g, cols].bitcast(FP8X4),
+                    rhs_scale=ws[:, g, cols],
+                    start=(g == 0),
+                    stop=(g == PASSES - 1),
+                )
+            u_t = ep.tile([P, 512], F32, name="u_t")
+            w_t = ep.tile([P, 512], F32, name="w_t")
+            if e == 0:
+                r_new = rp.tile([P, 4, 2, HD], F32, name="r_t")
+                r_tiles[b] = r_new
+            r_t = r_tiles[b]
+            nc.vector.tensor_tensor(out=u_t[:], in0=acc[:], in1=c4[:, e, :, :].rearrange("p h d -> p (h d)"), op=MULT)
+            nc.vector.tensor_tensor(out=w_t[:], in0=acc[:], in1=s4[:, e, :, :].rearrange("p h d -> p (h d)"), op=MULT)
+            nc.gpsimd.tensor_tensor(
+                out=r_t[:, :, e, :].rearrange("p h (i z) -> p h i z", z=2),
+                in0=u_t[:].rearrange("p (h i z) -> p h i z", h=4, z=2),
+                in1=w_t[:].rearrange("p (h i z) -> p h i z", h=4, z=2)[:, :, :, ::-1],
+                op=ADD,
+            )
+            if e == 1:
+                h0 = ((c % 2) * CHUNK + HALF * n) // HD
+                nc.sync.dma_start(
+                    out=outs[c // 2][b, h0 : h0 + 4, :, :].rearrange("h (p e) d -> p h (e d)", e=2),
+                    in_=r_t[:].rearrange("p h e d -> p h (e d)"),
+                )
+
+        groups = [(c, n) for c in range(N_CHUNKS) for n in range(2)]
+        prep_w(0, 0, 0)
+        prep_x(0, 0)
+        prep_x(0, 1)
+        prep_w(0, 0, 1)
+        prep_x(1, 0)
+        prep_x(1, 1)
+        prep_w(0, 0, 2)
+        prep_w(0, 0, 3)
+        for k in range(len(groups)):
+            c, n = groups[k]
+            for q in range(PASSES):
+                if k + 1 < len(groups):
+                    prep_w(groups[k + 1][0], groups[k + 1][1], q)
+                bank_work(c, n, q // 2, q % 2)

@@ -19,8 +19,10 @@ CHUNK = 1024
 HALF = 512
 N_CHUNKS = 2 * E // CHUNK
 PE_COLS = (256, 128)
-SCALAR_COLS = (224, 320)
+HEAD_UNITS = 2
+HEAD_VECTOR_COLS = 128
 RAW_BUFS = 8
+MM_AHEAD = 2
 
 FLOPS = 2 * B * S * D * 2 * E
 
@@ -35,45 +37,23 @@ def tile_llamaattention_pa_kernel(tc, x, Wq, Wk, rope_cos, rope_sin, out_0, out_
         xraw = ctx.enter_context(tc.tile_pool(name="xraw", bufs=2))
         xgrp = ctx.enter_context(tc.tile_pool(name="xgrp", bufs=2))
         wraw = ctx.enter_context(tc.tile_pool(name="wraw", bufs=RAW_BUFS))
-        wgrp = ctx.enter_context(tc.tile_pool(name="wgrp", bufs=4))
-        wcode = ctx.enter_context(tc.tile_pool(name="wcode", bufs=2))
-        ep = ctx.enter_context(tc.tile_pool(name="ep", bufs=4))
-        rp = ctx.enter_context(tc.tile_pool(name="rp", bufs=3))
+        wgrp = ctx.enter_context(tc.tile_pool(name="wgrp", bufs=3))
+        wcode = ctx.enter_context(tc.tile_pool(name="wcode", bufs=4))
+        ep = ctx.enter_context(tc.tile_pool(name="ep", bufs=3))
+        rp = ctx.enter_context(tc.tile_pool(name="rp", bufs=5))
         accp = ctx.enter_context(tc.psum_pool(name="accp", bufs=6))
         ptp = ctx.enter_context(tc.psum_pool(name="ptp", bufs=2))
 
         raw_tiles = {}
         x_tiles = {}
-
-        def w_rows(c, g, lo, hi):
-            w, j = c // 2, c % 2
-            return weights[w][512 * g : 512 * (g + 1), CHUNK * j + lo : CHUNK * j + hi].rearrange(
-                "(p t) c -> p t c", t=4
-            )
-
-        def new_raw(c, g):
-            raw = wraw.tile([P, 4, CHUNK], BF16, name="raw")
-            raw_tiles[(c, g)] = raw
-            return raw
-
-        def load_unit(c, g):
-            raw = new_raw(c, g)
-            nc.sync.dma_start(out=raw[:], in_=w_rows(c, g, 0, CHUNK))
-
-        def load_x(b):
-            x_sb = xraw.tile([P, 2, D], BF16, name="x_sb")
-            nc.sync.dma_start(out=x_sb[:], in_=x[b].rearrange("(p e) k -> p e k", e=2))
-            x_tiles[b] = x_sb
-
-        for g in range(PASSES):
-            raw = new_raw(0, g)
-            nc.sync.dma_start(out=raw[:, :, :HALF], in_=w_rows(0, g, 0, HALF))
-            if g < B:
-                load_x(g)
-        for g in range(PASSES):
-            nc.sync.dma_start(out=raw_tiles[(0, g)][:, :, HALF:], in_=w_rows(0, g, HALF, CHUNK))
-        for g in range(PASSES):
-            load_unit(1, g)
+        code_tiles = {}
+        grp_tiles = {}
+        pt_tiles = {}
+        acc_tiles = {}
+        r_tiles = {}
+        groups = [(c, n) for c in range(N_CHUNKS) for n in range(2)]
+        n_units = 2 * len(groups)
+        n_banks = 4 * len(groups)
 
         cos_sb = const.tile([P, 2, HD // 2], BF16, name="cos_sb")
         sin_sb = const.tile([P, 2, HD // 2], BF16, name="sin_sb")
@@ -90,20 +70,34 @@ def tile_llamaattention_pa_kernel(tc, x, Wq, Wk, rope_cos, rope_sin, out_0, out_
         nc.gpsimd.tensor_scalar(
             out=s2[:, :, :, 1:2], in0=sin_sb[:].unsqueeze(3), scalar1=-1.0, scalar2=0.0, op0=MULT, op1=ADD
         )
-        c4 = const.tile([P, 2, 4, HD], F32, name="c4")
-        s4 = const.tile([P, 2, 4, HD], F32, name="s4")
+        cs = const.tile([P, 2, 2, 4, HD], F32, name="cs")
         for e in range(2):
             nc.gpsimd.tensor_copy(
-                out=c4[:, e, :, :],
-                in_=c2[:, e, :, :].rearrange("p i e -> p (i e)").unsqueeze(1).to_broadcast([P, 4, HD]),
+                out=cs[:, e, 0, :, :],
+                in_=c2[:, e, :, :].rearrange("p i z -> p (i z)").unsqueeze(1).to_broadcast([P, 4, HD]),
             )
             nc.gpsimd.tensor_copy(
-                out=s4[:, e, :, :],
-                in_=s2[:, e, :, :].rearrange("p i e -> p (i e)").unsqueeze(1).to_broadcast([P, 4, HD]),
+                out=cs[:, e, 1, :, :],
+                in_=s2[:, e, :, :].rearrange("p i z -> p (i z)").unsqueeze(1).to_broadcast([P, 4, HD]),
             )
-
         xc = const.tile([P, 2 * B, 512], U32, name="xc", align_bytes=64)
         xs = const.tile([P, 2 * B, 512], U8, name="xs", align_bytes=64)
+
+        def w_rows(c, g, lo, hi):
+            w, j = c // 2, c % 2
+            return weights[w][512 * g : 512 * (g + 1), CHUNK * j + lo : CHUNK * j + hi].rearrange(
+                "(p t) c -> p t c", t=4
+            )
+
+        def load_unit(c, g):
+            raw = wraw.tile([P, 4, CHUNK], BF16, name="raw")
+            raw_tiles[(c, g)] = raw
+            nc.sync.dma_start(out=raw[:], in_=w_rows(c, g, 0, CHUNK))
+
+        def load_x(b):
+            x_sb = xraw.tile([P, 2, D], BF16, name="x_sb")
+            nc.sync.dma_start(out=x_sb[:], in_=x[b].rearrange("(p e) k -> p e k", e=2))
+            x_tiles[b] = x_sb
 
         def prep_x(b, e):
             m = 2 * b + e
@@ -111,7 +105,7 @@ def tile_llamaattention_pa_kernel(tc, x, Wq, Wk, rope_cos, rope_sin, out_0, out_
             xg = xgrp.tile([P, D], BF16, name="xg", align_bytes=64)
             xg_words = xg[:].bitcast(F32)
             for gp in range(2):
-                bank = ptp.tile([P, 2, 2, P], F32, name="bank", tag="pt")
+                bank = accp.tile([P, 2, 2, P], F32, name="bank", tag="acc")
                 for gg in range(2):
                     g = 2 * gp + gg
                     for u in range(2):
@@ -122,66 +116,104 @@ def tile_llamaattention_pa_kernel(tc, x, Wq, Wk, rope_cos, rope_sin, out_0, out_
                 )
             nc.vector.quantize_mx(out=xc[:, m, :].bitcast(FP8X4), scales=xs[:, m, :], in_=xg[:])
 
-        code_tiles = {}
+        def unit_src(unit, a):
+            k, gp = unit // 2, unit % 2
+            c, n = groups[k]
+            return raw_tiles[(c, 2 * gp + a)][:, :, HALF * n : HALF * (n + 1)]
 
-        def prep_w(c, n, g):
-            if (n, g) == (0, 0):
-                wc = wcode.tile([P, PASSES, CHUNK], U32, name="wc", align_bytes=64)
-                ws = wcode.tile([P, PASSES, CHUNK], U8, name="ws", align_bytes=64)
-                code_tiles[c] = (wc, ws)
-            wc, ws = code_tiles[c]
-            src = raw_tiles[(c, g)][:, :, HALF * n : HALF * (n + 1)]
-            grp = wgrp.tile([P, HALF, 4], BF16, name="grp", align_bytes=64)
-            pe_cols = PE_COLS[n]
-            s_end = pe_cols + SCALAR_COLS[n]
-            pt = ptp.tile([P, 256, 4], BF16, name="pt", tag="pt")
-            for c1 in range(0, pe_cols, P):
-                nc.tensor.matmul(
-                    out=pt[:, c1 : c1 + P, :],
-                    lhsT=ident_bf[:],
-                    rhs=src[:, :, c1 : c1 + P].rearrange("p t c -> p c t"),
-                    start=True,
-                    stop=True,
-                )
-            nc.scalar.copy(out=grp[:, :pe_cols, :], in_=pt[:, :pe_cols, :])
-            nc.scalar.copy(out=grp[:, pe_cols:s_end, :], in_=src[:, :, pe_cols:s_end].rearrange("p t c -> p c t"))
-            nc.vector.tensor_copy(out=grp[:, s_end:, :], in_=src[:, :, s_end:].rearrange("p t c -> p c t"))
-            cols = slice(HALF * n, HALF * (n + 1))
-            nc.vector.quantize_mx(
-                out=wc[:, g, cols].bitcast(FP8X4), scales=ws[:, g, cols], in_=grp[:].rearrange("p c t -> p (c t)")
+        def weave(dst, src):
+            return (
+                dst.rearrange("p (c i) t -> p c t i", i=4),
+                src.rearrange("p t (c i) -> p c t i", i=4),
             )
+
+        def pass_through(unit):
+            for a in range(2):
+                src = unit_src(unit, a)
+                pt = ptp.tile([P, 256, 4], BF16, name="pt", tag="pt")
+                pt_tiles[(unit, a)] = pt
+                for c1 in range(0, PE_COLS[a], P):
+                    nc.tensor.matmul(
+                        out=pt[:, c1 : c1 + P, :],
+                        lhsT=ident_bf[:],
+                        rhs=src[:, :, c1 : c1 + P].rearrange("p t c -> p c t"),
+                        start=True,
+                        stop=True,
+                    )
+
+        def direct_copies(unit):
+            grp = wgrp.tile([P, 2, HALF, 4], BF16, name="grp", align_bytes=64)
+            grp_tiles[unit] = grp
+            v_cols = HEAD_VECTOR_COLS if unit < HEAD_UNITS else 0
+            s_end = HALF - v_cols
+            for a in range(2):
+                src = unit_src(unit, a)
+                dst = grp[:, a, :, :]
+                o_ap, i_ap = weave(dst[:, PE_COLS[a] : s_end, :], src[:, :, PE_COLS[a] : s_end])
+                nc.scalar.copy(out=o_ap, in_=i_ap)
+                if v_cols:
+                    o_ap, i_ap = weave(dst[:, s_end:, :], src[:, :, s_end:])
+                    nc.vector.tensor_copy(out=o_ap, in_=i_ap)
+
+        def empty_pass_through(unit):
+            k, gp = unit // 2, unit % 2
+            c, n = groups[k]
+            for a in range(2):
+                nc.scalar.copy(
+                    out=grp_tiles[unit][:, a, : PE_COLS[a], :], in_=pt_tiles[(unit, a)][:, : PE_COLS[a], :]
+                )
             if n == 1 and c + 2 < N_CHUNKS:
-                load_unit(c + 2, g)
+                load_unit(c + 2, 2 * gp)
+                load_unit(c + 2, 2 * gp + 1)
 
-        r_tiles = {}
+        def quantise(unit):
+            k, gp = unit // 2, unit % 2
+            if gp == 0:
+                wc = wcode.tile([P, PASSES, HALF], U32, name="wc", align_bytes=64)
+                ws = wcode.tile([P, PASSES, HALF], U8, name="ws", align_bytes=64)
+                code_tiles[k] = (wc, ws)
+            wc, ws = code_tiles[k]
+            nc.vector.quantize_mx(
+                out=wc[:, 2 * gp : 2 * gp + 2, :].rearrange("p g c -> p (g c)").bitcast(FP8X4),
+                scales=ws[:, 2 * gp : 2 * gp + 2, :].rearrange("p g c -> p (g c)"),
+                in_=grp_tiles[unit][:].rearrange("p a c t -> p (a c t)"),
+            )
 
-        def bank_work(c, n, b, e):
-            wc, ws = code_tiles[c]
-            m = 2 * b + e
-            cols = slice(HALF * n, HALF * (n + 1))
-            acc = accp.tile([P, 512], F32, name="acc")
+        def matmuls(bank):
+            k, m = bank // 4, bank % 4
+            wc, ws = code_tiles[k]
+            acc = accp.tile([P, 512], F32, name="acc", tag="acc")
+            acc_tiles[bank] = acc
             for g in range(PASSES):
                 nc.tensor.matmul_mx(
                     out=acc[:],
                     lhsT=xc[:, m, P * g : P * (g + 1)].bitcast(FP8X4),
                     lhsT_scale=xs[:, m, P * g : P * (g + 1)],
-                    rhs=wc[:, g, cols].bitcast(FP8X4),
-                    rhs_scale=ws[:, g, cols],
+                    rhs=wc[:, g, :].bitcast(FP8X4),
+                    rhs_scale=ws[:, g, :],
                     start=(g == 0),
                     stop=(g == PASSES - 1),
                 )
-            u_t = ep.tile([P, 512], F32, name="u_t")
-            w_t = ep.tile([P, 512], F32, name="w_t")
+
+        def rotate(bank):
+            k, m = bank // 4, bank % 4
+            c, n = groups[k]
+            b, e = m // 2, m % 2
+            uw = ep.tile([P, 2, 512], F32, name="uw")
             if e == 0:
                 r_new = rp.tile([P, 4, 2, HD], F32, name="r_t")
                 r_tiles[b] = r_new
             r_t = r_tiles[b]
-            nc.vector.tensor_tensor(out=u_t[:], in0=acc[:], in1=c4[:, e, :, :].rearrange("p h d -> p (h d)"), op=MULT)
-            nc.vector.tensor_tensor(out=w_t[:], in0=acc[:], in1=s4[:, e, :, :].rearrange("p h d -> p (h d)"), op=MULT)
+            nc.vector.tensor_tensor(
+                out=uw[:],
+                in0=acc_tiles[bank][:].unsqueeze(1).to_broadcast([P, 2, 512]),
+                in1=cs[:, e, :, :, :].rearrange("p f h d -> p f (h d)"),
+                op=MULT,
+            )
             nc.gpsimd.tensor_tensor(
                 out=r_t[:, :, e, :].rearrange("p h (i z) -> p h i z", z=2),
-                in0=u_t[:].rearrange("p (h i z) -> p h i z", h=4, z=2),
-                in1=w_t[:].rearrange("p (h i z) -> p h i z", h=4, z=2)[:, :, :, ::-1],
+                in0=uw[:, 0, :].rearrange("p (h i z) -> p h i z", h=4, z=2),
+                in1=uw[:, 1, :].rearrange("p (h i z) -> p h i z", h=4, z=2)[:, :, :, ::-1],
                 op=ADD,
             )
             if e == 1:
@@ -191,18 +223,43 @@ def tile_llamaattention_pa_kernel(tc, x, Wq, Wk, rope_cos, rope_sin, out_0, out_
                     in_=r_t[:].rearrange("p h e d -> p h (e d)"),
                 )
 
-        groups = [(c, n) for c in range(N_CHUNKS) for n in range(2)]
-        prep_w(0, 0, 0)
-        prep_x(0, 0)
-        prep_x(0, 1)
-        prep_w(0, 0, 1)
-        prep_x(1, 0)
-        prep_x(1, 1)
-        prep_w(0, 0, 2)
-        prep_w(0, 0, 3)
-        for k in range(len(groups)):
-            c, n = groups[k]
-            for q in range(PASSES):
-                if k + 1 < len(groups):
-                    prep_w(groups[k + 1][0], groups[k + 1][1], q)
-                bank_work(c, n, q // 2, q % 2)
+        with tc.manual_schedule():
+            load_x(0)
+            load_x(1)
+            for g in range(PASSES):
+                raw = wraw.tile([P, 4, CHUNK], BF16, name="raw")
+                raw_tiles[(0, g)] = raw
+                nc.sync.dma_start(out=raw[:, :, :HALF], in_=w_rows(0, g, 0, HALF))
+            for g in range(PASSES):
+                nc.sync.dma_start(out=raw_tiles[(0, g)][:, :, HALF:], in_=w_rows(0, g, HALF, CHUNK))
+            for g in range(PASSES):
+                load_unit(1, g)
+            for m in range(2 * B):
+                prep_x(m // 2, m % 2)
+            pass_through(0)
+            progress = [0, 0]
+            for step in range(n_units + 3):
+                if step < n_units:
+                    direct_copies(step)
+                    empty_pass_through(step)
+                if 1 <= step <= n_units:
+                    quantise(step - 1)
+                ready = min(4 * (step // 2), n_banks)
+                if step < 2:
+                    turns = 0
+                elif step == 2:
+                    turns = 1
+                elif step <= n_units:
+                    turns = 2
+                else:
+                    turns = 4
+                for turn in range(turns):
+                    while progress[0] < min(ready, progress[1] + MM_AHEAD + 1):
+                        matmuls(progress[0])
+                        progress[0] = progress[0] + 1
+                    if progress[1] < progress[0]:
+                        rotate(progress[1])
+                        progress[1] = progress[1] + 1
+                if step + 1 < n_units:
+                    pass_through(step + 1)
+            assert progress[1] == n_banks

@@ -122,10 +122,7 @@ def tile_llamaattention_pa_kernel(tc, x, Wq, Wk, rope_cos, rope_sin, out_0, out_
             return raw_tiles[(c, 2 * gp + a)][:, :, HALF * n : HALF * (n + 1)]
 
         def weave(dst, src):
-            return (
-                dst.rearrange("p (c i) t -> p c t i", i=4),
-                src.rearrange("p t (c i) -> p c t i", i=4),
-            )
+            return (dst, src.rearrange("p t c -> p c t"))
 
         def pass_through(unit):
             for a in range(2):

@@ -39,7 +39,7 @@ def tile_llamaattention_pa_kernel(tc, x, Wq, Wk, rope_cos, rope_sin, out_0, out_
         wraw = ctx.enter_context(tc.tile_pool(name="wraw", bufs=RAW_BUFS))
         wgrp = ctx.enter_context(tc.tile_pool(name="wgrp", bufs=3))
         wcode = ctx.enter_context(tc.tile_pool(name="wcode", bufs=4))
-        ep = ctx.enter_context(tc.tile_pool(name="ep", bufs=3))
+        ep = ctx.enter_context(tc.tile_pool(name="ep", bufs=5))
         rp = ctx.enter_context(tc.tile_pool(name="rp", bufs=5))
         accp = ctx.enter_context(tc.psum_pool(name="accp", bufs=6))
         ptp = ctx.enter_context(tc.psum_pool(name="ptp", bufs=2))
@@ -51,6 +51,7 @@ def tile_llamaattention_pa_kernel(tc, x, Wq, Wk, rope_cos, rope_sin, out_0, out_
         pt_tiles = {}
         acc_tiles = {}
         r_tiles = {}
+        uw_tiles = {}
         groups = [(c, n) for c in range(N_CHUNKS) for n in range(2)]
         n_units = 2 * len(groups)
         n_banks = 4 * len(groups)
@@ -197,17 +198,24 @@ def tile_llamaattention_pa_kernel(tc, x, Wq, Wk, rope_cos, rope_sin, out_0, out_
             c, n = groups[k]
             b, e = m // 2, m % 2
             uw = ep.tile([P, 2, 512], F32, name="uw")
+            uw_tiles[bank] = uw
             if e == 0:
                 r_new = rp.tile([P, 4, 2, HD], F32, name="r_t")
-                r_tiles[b] = r_new
-            r_t = r_tiles[b]
+                r_tiles[bank // 2] = r_new
             nc.vector.tensor_tensor(
                 out=uw[:],
                 in0=acc_tiles[bank][:].unsqueeze(1).to_broadcast([P, 2, 512]),
                 in1=cs[:, e, :, :, :].rearrange("p f h d -> p f (h d)"),
                 op=MULT,
             )
-            nc.gpsimd.tensor_tensor(
+
+        def combine(bank, engine):
+            k, m = bank // 4, bank % 4
+            c, n = groups[k]
+            b, e = m // 2, m % 2
+            uw = uw_tiles[bank]
+            r_t = r_tiles[bank // 2]
+            engine.tensor_tensor(
                 out=r_t[:, :, e, :].rearrange("p h (i z) -> p h i z", z=2),
                 in0=uw[:, 0, :].rearrange("p (h i z) -> p h i z", h=4, z=2),
                 in1=uw[:, 1, :].rearrange("p (h i z) -> p h i z", h=4, z=2)[:, :, :, ::-1],
@@ -235,12 +243,16 @@ def tile_llamaattention_pa_kernel(tc, x, Wq, Wk, rope_cos, rope_sin, out_0, out_
                 prep_x(m // 2, m % 2)
             pass_through(0)
             progress = [0, 0]
+            pending = []
             for step in range(n_units + 3):
                 if step < n_units:
                     direct_copies(step)
                     empty_pass_through(step)
                 if 1 <= step <= n_units:
                     quantise(step - 1)
+                for bank in pending:
+                    combine(bank, nc.vector)
+                pending.clear()
                 ready = min(4 * (step // 2), n_banks)
                 if step < 2:
                     turns = 0
@@ -256,6 +268,12 @@ def tile_llamaattention_pa_kernel(tc, x, Wq, Wk, rope_cos, rope_sin, out_0, out_
                         progress[0] = progress[0] + 1
                     if progress[1] < progress[0]:
                         rotate(progress[1])
+                        if progress[1] % 2 == 0:
+                            combine(progress[1], nc.gpsimd)
+                        elif step < n_units:
+                            pending.append(progress[1])
+                        else:
+                            combine(progress[1], nc.vector)
                         progress[1] = progress[1] + 1
                 if step + 1 < n_units:
                     pass_through(step + 1)

@@ -18,13 +18,24 @@ PASSES = D // 512
 CHUNK = 1024
 HALF = 512
 N_CHUNKS = 2 * E // CHUNK
+TOKEN_TILES = B * S // P
+
 PE_COLS = (256, 128)
-HEAD_UNITS = 2
-HEAD_VECTOR_COLS = 128
+HEAD_VECTOR_COLS = ((128, 128), (128, 128), (0, 64), (0, 64))
 RAW_BUFS = 8
 MM_AHEAD = 2
 
 FLOPS = 2 * B * S * D * 2 * E
+
+
+def rotations_in(step, n_units):
+    if step < 2:
+        return 0
+    if step == 2:
+        return 1
+    if step <= n_units:
+        return 2
+    return 4
 
 
 def tile_llamaattention_pa_kernel(tc, x, Wq, Wk, rope_cos, rope_sin, out_0, out_1):
@@ -39,7 +50,7 @@ def tile_llamaattention_pa_kernel(tc, x, Wq, Wk, rope_cos, rope_sin, out_0, out_
         wraw = ctx.enter_context(tc.tile_pool(name="wraw", bufs=RAW_BUFS))
         wgrp = ctx.enter_context(tc.tile_pool(name="wgrp", bufs=3))
         wcode = ctx.enter_context(tc.tile_pool(name="wcode", bufs=4))
-        ep = ctx.enter_context(tc.tile_pool(name="ep", bufs=5))
+        ep = ctx.enter_context(tc.tile_pool(name="ep", bufs=3))
         rp = ctx.enter_context(tc.tile_pool(name="rp", bufs=5))
         accp = ctx.enter_context(tc.psum_pool(name="accp", bufs=6))
         ptp = ctx.enter_context(tc.psum_pool(name="ptp", bufs=2))
@@ -51,10 +62,9 @@ def tile_llamaattention_pa_kernel(tc, x, Wq, Wk, rope_cos, rope_sin, out_0, out_
         pt_tiles = {}
         acc_tiles = {}
         r_tiles = {}
-        uw_tiles = {}
         groups = [(c, n) for c in range(N_CHUNKS) for n in range(2)]
         n_units = 2 * len(groups)
-        n_banks = 4 * len(groups)
+        n_banks = TOKEN_TILES * len(groups)
 
         cos_sb = const.tile([P, 2, HD // 2], BF16, name="cos_sb")
         sin_sb = const.tile([P, 2, HD // 2], BF16, name="sin_sb")
@@ -81,8 +91,8 @@ def tile_llamaattention_pa_kernel(tc, x, Wq, Wk, rope_cos, rope_sin, out_0, out_
                 out=cs[:, e, 1, :, :],
                 in_=s2[:, e, :, :].rearrange("p i z -> p (i z)").unsqueeze(1).to_broadcast([P, 4, HD]),
             )
-        xc = const.tile([P, 2 * B, 512], U32, name="xc", align_bytes=64)
-        xs = const.tile([P, 2 * B, 512], U8, name="xs", align_bytes=64)
+        xc = const.tile([P, TOKEN_TILES, 512], U32, name="xc", align_bytes=64)
+        xs = const.tile([P, TOKEN_TILES, 512], U8, name="xs", align_bytes=64)
 
         def w_rows(c, g, lo, hi):
             w, j = c // 2, c % 2
@@ -122,9 +132,6 @@ def tile_llamaattention_pa_kernel(tc, x, Wq, Wk, rope_cos, rope_sin, out_0, out_
             c, n = groups[k]
             return raw_tiles[(c, 2 * gp + a)][:, :, HALF * n : HALF * (n + 1)]
 
-        def weave(dst, src):
-            return (dst, src.rearrange("p t c -> p c t"))
-
         def pass_through(unit):
             for a in range(2):
                 src = unit_src(unit, a)
@@ -142,16 +149,16 @@ def tile_llamaattention_pa_kernel(tc, x, Wq, Wk, rope_cos, rope_sin, out_0, out_
         def direct_copies(unit):
             grp = wgrp.tile([P, 2, HALF, 4], BF16, name="grp", align_bytes=64)
             grp_tiles[unit] = grp
-            v_cols = HEAD_VECTOR_COLS if unit < HEAD_UNITS else 0
-            s_end = HALF - v_cols
             for a in range(2):
+                v_cols = HEAD_VECTOR_COLS[unit][a] if unit < len(HEAD_VECTOR_COLS) else 0
+                s_end = HALF - v_cols
                 src = unit_src(unit, a)
                 dst = grp[:, a, :, :]
-                o_ap, i_ap = weave(dst[:, PE_COLS[a] : s_end, :], src[:, :, PE_COLS[a] : s_end])
-                nc.scalar.copy(out=o_ap, in_=i_ap)
+                nc.scalar.copy(
+                    out=dst[:, PE_COLS[a] : s_end, :], in_=src[:, :, PE_COLS[a] : s_end].rearrange("p t c -> p c t")
+                )
                 if v_cols:
-                    o_ap, i_ap = weave(dst[:, s_end:, :], src[:, :, s_end:])
-                    nc.vector.tensor_copy(out=o_ap, in_=i_ap)
+                    nc.vector.tensor_copy(out=dst[:, s_end:, :], in_=src[:, :, s_end:].rearrange("p t c -> p c t"))
 
         def empty_pass_through(unit):
             k, gp = unit // 2, unit % 2
@@ -178,7 +185,7 @@ def tile_llamaattention_pa_kernel(tc, x, Wq, Wk, rope_cos, rope_sin, out_0, out_
             )
 
         def matmuls(bank):
-            k, m = bank // 4, bank % 4
+            k, m = bank // TOKEN_TILES, bank % TOKEN_TILES
             wc, ws = code_tiles[k]
             acc = accp.tile([P, 512], F32, name="acc", tag="acc")
             acc_tiles[bank] = acc
@@ -194,28 +201,22 @@ def tile_llamaattention_pa_kernel(tc, x, Wq, Wk, rope_cos, rope_sin, out_0, out_
                 )
 
         def rotate(bank):
-            k, m = bank // 4, bank % 4
+            k, m = bank // TOKEN_TILES, bank % TOKEN_TILES
             c, n = groups[k]
             b, e = m // 2, m % 2
             uw = ep.tile([P, 2, 512], F32, name="uw")
-            uw_tiles[bank] = uw
             if e == 0:
                 r_new = rp.tile([P, 4, 2, HD], F32, name="r_t")
-                r_tiles[bank // 2] = r_new
+                r_tiles[b] = r_new
+            r_t = r_tiles[b]
             nc.vector.tensor_tensor(
                 out=uw[:],
                 in0=acc_tiles[bank][:].unsqueeze(1).to_broadcast([P, 2, 512]),
                 in1=cs[:, e, :, :, :].rearrange("p f h d -> p f (h d)"),
                 op=MULT,
             )
-
-        def combine(bank, engine):
-            k, m = bank // 4, bank % 4
-            c, n = groups[k]
-            b, e = m // 2, m % 2
-            uw = uw_tiles[bank]
-            r_t = r_tiles[bank // 2]
-            engine.tensor_tensor(
+            adder = nc.vector if bank == n_banks - 1 else nc.gpsimd
+            adder.tensor_tensor(
                 out=r_t[:, :, e, :].rearrange("p h (i z) -> p h i z", z=2),
                 in0=uw[:, 0, :].rearrange("p (h i z) -> p h i z", h=4, z=2),
                 in1=uw[:, 1, :].rearrange("p (h i z) -> p h i z", h=4, z=2)[:, :, :, ::-1],
@@ -239,42 +240,25 @@ def tile_llamaattention_pa_kernel(tc, x, Wq, Wk, rope_cos, rope_sin, out_0, out_
                 nc.sync.dma_start(out=raw_tiles[(0, g)][:, :, HALF:], in_=w_rows(0, g, HALF, CHUNK))
             for g in range(PASSES):
                 load_unit(1, g)
-            for m in range(2 * B):
+            for m in range(TOKEN_TILES):
                 prep_x(m // 2, m % 2)
             pass_through(0)
-            progress = [0, 0]
-            pending = []
-            for step in range(n_units + 3):
+            multiplied = 0
+            rotated = 0
+            for step in range(n_units + 2):
                 if step < n_units:
                     direct_copies(step)
                     empty_pass_through(step)
                 if 1 <= step <= n_units:
                     quantise(step - 1)
-                for bank in pending:
-                    combine(bank, nc.vector)
-                pending.clear()
-                ready = min(4 * (step // 2), n_banks)
-                if step < 2:
-                    turns = 0
-                elif step == 2:
-                    turns = 1
-                elif step <= n_units:
-                    turns = 2
-                else:
-                    turns = 4
-                for turn in range(turns):
-                    while progress[0] < min(ready, progress[1] + MM_AHEAD + 1):
-                        matmuls(progress[0])
-                        progress[0] = progress[0] + 1
-                    if progress[1] < progress[0]:
-                        rotate(progress[1])
-                        if progress[1] % 2 == 0:
-                            combine(progress[1], nc.gpsimd)
-                        elif step < n_units:
-                            pending.append(progress[1])
-                        else:
-                            combine(progress[1], nc.vector)
-                        progress[1] = progress[1] + 1
+                ready = min(TOKEN_TILES * (step // 2), n_banks)
+                for turn in range(rotations_in(step, n_units)):
+                    while multiplied < min(ready, rotated + MM_AHEAD + 1):
+                        matmuls(multiplied)
+                        multiplied = multiplied + 1
+                    if rotated < multiplied:
+                        rotate(rotated)
+                        rotated = rotated + 1
                 if step + 1 < n_units:
                     pass_through(step + 1)
-            assert progress[1] == n_banks
+            assert rotated == n_banks

@@ -76,21 +76,26 @@ def tile_llamaattention_pa_kernel(tc, x, Wq, Wk, rope_cos, rope_sin, out_0, out_
         make_identity(nc, ident_bf[:])
         c2 = const.tile([P, 2, HD // 2, 2], F32, name="c2")
         s2 = const.tile([P, 2, HD // 2, 2], F32, name="s2")
-        nc.gpsimd.tensor_copy(out=c2[:], in_=cos_sb[:].unsqueeze(3).to_broadcast([P, 2, HD // 2, 2]))
-        nc.gpsimd.tensor_copy(out=s2[:, :, :, 0:1], in_=sin_sb[:].unsqueeze(3))
+        nc.gpsimd.tensor_scalar(
+            out=c2[:], in0=cos_sb[:].unsqueeze(3).to_broadcast([P, 2, HD // 2, 2]), scalar1=1.0, scalar2=0.0, op0=MULT, op1=ADD
+        )
+        nc.gpsimd.tensor_scalar(
+            out=s2[:, :, :, 0:1], in0=sin_sb[:].unsqueeze(3), scalar1=1.0, scalar2=0.0, op0=MULT, op1=ADD
+        )
         nc.gpsimd.tensor_scalar(
             out=s2[:, :, :, 1:2], in0=sin_sb[:].unsqueeze(3), scalar1=-1.0, scalar2=0.0, op0=MULT, op1=ADD
         )
         cs = const.tile([P, 2, 2, 4, HD], F32, name="cs")
         for e in range(2):
-            nc.gpsimd.tensor_copy(
-                out=cs[:, e, 0, :, :],
-                in_=c2[:, e, :, :].rearrange("p i z -> p (i z)").unsqueeze(1).to_broadcast([P, 4, HD]),
-            )
-            nc.gpsimd.tensor_copy(
-                out=cs[:, e, 1, :, :],
-                in_=s2[:, e, :, :].rearrange("p i z -> p (i z)").unsqueeze(1).to_broadcast([P, 4, HD]),
-            )
+            for f, table in enumerate((c2, s2)):
+                nc.gpsimd.tensor_scalar(
+                    out=cs[:, e, f, :, :],
+                    in0=table[:, e, :, :].rearrange("p i z -> p (i z)").unsqueeze(1).to_broadcast([P, 4, HD]),
+                    scalar1=1.0,
+                    scalar2=0.0,
+                    op0=MULT,
+                    op1=ADD,
+                )
         xc = const.tile([P, TOKEN_TILES, 512], U32, name="xc", align_bytes=64)
         xs = const.tile([P, TOKEN_TILES, 512], U8, name="xs", align_bytes=64)
 

@@ -23,19 +23,9 @@ TOKEN_TILES = B * S // P
 PE_COLS = (256, 128)
 HEAD_VECTOR_COLS = ((128, 128), (128, 128), (0, 64), (0, 64))
 RAW_BUFS = 8
-MM_AHEAD = 2
+LAG = 3
 
 FLOPS = 2 * B * S * D * 2 * E
-
-
-def rotations_in(step, n_units):
-    if step < 2:
-        return 0
-    if step == 2:
-        return 1
-    if step <= n_units:
-        return 2
-    return 4
 
 
 def tile_llamaattention_pa_kernel(tc, x, Wq, Wk, rope_cos, rope_sin, out_0, out_1):
@@ -62,6 +52,7 @@ def tile_llamaattention_pa_kernel(tc, x, Wq, Wk, rope_cos, rope_sin, out_0, out_
         pt_tiles = {}
         acc_tiles = {}
         r_tiles = {}
+        uw_tiles = {}
         groups = [(c, n) for c in range(N_CHUNKS) for n in range(2)]
         n_units = 2 * len(groups)
         n_banks = TOKEN_TILES * len(groups)
@@ -168,10 +159,8 @@ def tile_llamaattention_pa_kernel(tc, x, Wq, Wk, rope_cos, rope_sin, out_0, out_
         def empty_pass_through(unit):
             k, gp = unit // 2, unit % 2
             c, n = groups[k]
-            for a in range(2):
-                nc.scalar.copy(
-                    out=grp_tiles[unit][:, a, : PE_COLS[a], :], in_=pt_tiles[(unit, a)][:, : PE_COLS[a], :]
-                )
+            nc.scalar.copy(out=grp_tiles[unit][:, 0, : PE_COLS[0], :], in_=pt_tiles[(unit, 0)][:, : PE_COLS[0], :])
+            nc.vector.tensor_copy(out=grp_tiles[unit][:, 1, : PE_COLS[1], :], in_=pt_tiles[(unit, 1)][:, : PE_COLS[1], :])
             if n == 1 and c + 2 < N_CHUNKS:
                 load_unit(c + 2, 2 * gp)
                 load_unit(c + 2, 2 * gp + 1)
@@ -209,24 +198,34 @@ def tile_llamaattention_pa_kernel(tc, x, Wq, Wk, rope_cos, rope_sin, out_0, out_
             k, m = bank // TOKEN_TILES, bank % TOKEN_TILES
             c, n = groups[k]
             b, e = m // 2, m % 2
-            uw = ep.tile([P, 2, 512], F32, name="uw")
             if e == 0:
+                uw_new = ep.tile([P, 2, 4, 2, HD], F32, name="uw")
+                uw_tiles[b] = uw_new
                 r_new = rp.tile([P, 4, 2, HD], F32, name="r_t")
                 r_tiles[b] = r_new
+            uw = uw_tiles[b]
             r_t = r_tiles[b]
             nc.vector.tensor_tensor(
-                out=uw[:],
-                in0=acc_tiles[bank][:].unsqueeze(1).to_broadcast([P, 2, 512]),
-                in1=cs[:, e, :, :, :].rearrange("p f h d -> p f (h d)"),
+                out=uw[:, :, :, e, :],
+                in0=acc_tiles[bank][:].rearrange("p (h d) -> p h d", h=4).unsqueeze(1).to_broadcast([P, 2, 4, HD]),
+                in1=cs[:, e, :, :, :],
                 op=MULT,
             )
-            adder = nc.vector if bank == n_banks - 1 else nc.gpsimd
-            adder.tensor_tensor(
-                out=r_t[:, :, e, :].rearrange("p h (i z) -> p h i z", z=2),
-                in0=uw[:, 0, :].rearrange("p (h i z) -> p h i z", h=4, z=2),
-                in1=uw[:, 1, :].rearrange("p (h i z) -> p h i z", h=4, z=2)[:, :, :, ::-1],
-                op=ADD,
-            )
+            if k == len(groups) - 1 and b == B - 1:
+                adder = nc.vector if e == 1 else nc.gpsimd
+                adder.tensor_tensor(
+                    out=r_t[:, :, e, :].rearrange("p h (i z) -> p h i z", z=2),
+                    in0=uw[:, 0, :, e, :].rearrange("p h (i z) -> p h i z", z=2),
+                    in1=uw[:, 1, :, e, :].rearrange("p h (i z) -> p h i z", z=2)[:, :, :, ::-1],
+                    op=ADD,
+                )
+            elif e == 1:
+                nc.gpsimd.tensor_tensor(
+                    out=r_t[:].rearrange("p h e (i z) -> p (h e i) z", z=2),
+                    in0=uw[:, 0, :, :, :].rearrange("p h e (i z) -> p (h e i) z", z=2),
+                    in1=uw[:, 1, :, :, :].rearrange("p h e (i z) -> p (h e i) z", z=2)[:, :, ::-1],
+                    op=ADD,
+                )
             if e == 1:
                 h0 = ((c % 2) * CHUNK + HALF * n) // HD
                 nc.sync.dma_start(
@@ -248,22 +247,21 @@ def tile_llamaattention_pa_kernel(tc, x, Wq, Wk, rope_cos, rope_sin, out_0, out_
             for m in range(TOKEN_TILES):
                 prep_x(m // 2, m % 2)
             pass_through(0)
-            multiplied = 0
-            rotated = 0
-            for step in range(n_units + 2):
+            n_pairs = n_banks // 2
+            for step in range(n_units + LAG):
                 if step < n_units:
                     direct_copies(step)
                     empty_pass_through(step)
-                if 1 <= step <= n_units:
-                    quantise(step - 1)
-                ready = min(TOKEN_TILES * (step // 2), n_banks)
-                for turn in range(rotations_in(step, n_units)):
-                    while multiplied < min(ready, rotated + MM_AHEAD + 1):
-                        matmuls(multiplied)
-                        multiplied = multiplied + 1
-                    if rotated < multiplied:
-                        rotate(rotated)
-                        rotated = rotated + 1
                 if step + 1 < n_units:
                     pass_through(step + 1)
-            assert rotated == n_banks
+                pair = step - LAG
+                if pair >= 0:
+                    rotate(2 * pair)
+                    rotate(2 * pair + 1)
+                if step < n_units:
+                    quantise(step)
+                nxt = pair + 1
+                if 0 <= nxt < n_pairs:
+                    assert 2 * (nxt // 2) + 1 <= step
+                    matmuls(2 * nxt)
+                    matmuls(2 * nxt + 1)

@@ -20,7 +20,7 @@ HALF = 512
 N_CHUNKS = 2 * E // CHUNK
 TOKEN_TILES = B * S // P
 
-PE_COLS = (256, 128)
+PE_COLS = (192, 128)
 HEAD_VECTOR_COLS = ((128, 128), (128, 128), (0, 64), (0, 64))
 RAW_BUFS = 8
 LAG = 3
@@ -134,10 +134,11 @@ def tile_llamaattention_pa_kernel(tc, x, Wq, Wk, rope_cos, rope_sin, out_0, out_
                 pt = ptp.tile([P, 256, 4], BF16, name="pt", tag="pt")
                 pt_tiles[(unit, a)] = pt
                 for c1 in range(0, PE_COLS[a], P):
+                    c_end = min(c1 + P, PE_COLS[a])
                     nc.tensor.matmul(
-                        out=pt[:, c1 : c1 + P, :],
+                        out=pt[:, c1:c_end, :],
                         lhsT=ident_bf[:],
-                        rhs=src[:, :, c1 : c1 + P].rearrange("p t c -> p c t"),
+                        rhs=src[:, :, c1:c_end].rearrange("p t c -> p c t"),
                         start=True,
                         stop=True,
                     )

@@ -136,9 +136,9 @@ def tile_llamaattention_pa_kernel(tc, x, Wq, Wk, rope_cos, rope_sin, out_0, out_
                 for c1 in range(0, PE_COLS[a], P):
                     c_end = min(c1 + P, PE_COLS[a])
                     nc.tensor.matmul(
-                        out=pt[:, c1:c_end, :],
+                        out=pt[:, c1:c_end, :].rearrange("p c t -> p t c"),
                         lhsT=ident_bf[:],
-                        rhs=src[:, :, c1:c_end].rearrange("p t c -> p c t"),
+                        rhs=src[:, :, c1:c_end],
                         start=True,
                         stop=True,
                     )

@@ -20,9 +20,10 @@ HALF = 512
 N_CHUNKS = 2 * E // CHUNK
 TOKEN_TILES = B * S // P
 
-PE_COLS = (192, 128)
-HEAD_VECTOR_COLS = ((128, 128), (128, 128), (0, 64), (0, 64))
+PE_COLS = (256, 128)
+HEAD_VECTOR_COLS = ((0, 128), (0, 128))
 RAW_BUFS = 8
+CHUNKS_IN_HALVES = 2
 LAG = 3
 
 FLOPS = 2 * B * S * D * 2 * E
@@ -42,20 +43,20 @@ def tile_llamaattention_pa_kernel(tc, x, Wq, Wk, rope_cos, rope_sin, out_0, out_
         wcode = ctx.enter_context(tc.tile_pool(name="wcode", bufs=4))
         ep = ctx.enter_context(tc.tile_pool(name="ep", bufs=3))
         rp = ctx.enter_context(tc.tile_pool(name="rp", bufs=5))
-        accp = ctx.enter_context(tc.psum_pool(name="accp", bufs=6))
-        ptp = ctx.enter_context(tc.psum_pool(name="ptp", bufs=2))
+        accp = ctx.enter_context(tc.psum_pool(name="accp", bufs=4))
+        ptp = ctx.enter_context(tc.psum_pool(name="ptp", bufs=4))
 
         raw_tiles = {}
         x_tiles = {}
+        xbank_tiles = {}
+        xg_tiles = {}
         code_tiles = {}
         grp_tiles = {}
         pt_tiles = {}
         acc_tiles = {}
-        r_tiles = {}
-        uw_tiles = {}
         groups = [(c, n) for c in range(N_CHUNKS) for n in range(2)]
         n_units = 2 * len(groups)
-        n_banks = TOKEN_TILES * len(groups)
+        n_pairs = B * len(groups)
 
         cos_sb = const.tile([P, 2, HD // 2], BF16, name="cos_sb")
         sin_sb = const.tile([P, 2, HD // 2], BF16, name="sin_sb")
@@ -67,61 +68,59 @@ def tile_llamaattention_pa_kernel(tc, x, Wq, Wk, rope_cos, rope_sin, out_0, out_
         make_identity(nc, ident_bf[:])
         c2 = const.tile([P, 2, HD // 2, 2], F32, name="c2")
         s2 = const.tile([P, 2, HD // 2, 2], F32, name="s2")
-        nc.gpsimd.tensor_scalar(
-            out=c2[:], in0=cos_sb[:].unsqueeze(3).to_broadcast([P, 2, HD // 2, 2]), scalar1=1.0, scalar2=0.0, op0=MULT, op1=ADD
-        )
-        nc.gpsimd.tensor_scalar(
-            out=s2[:, :, :, 0:1], in0=sin_sb[:].unsqueeze(3), scalar1=1.0, scalar2=0.0, op0=MULT, op1=ADD
-        )
-        nc.gpsimd.tensor_scalar(
-            out=s2[:, :, :, 1:2], in0=sin_sb[:].unsqueeze(3), scalar1=-1.0, scalar2=0.0, op0=MULT, op1=ADD
-        )
+        nc.scalar.copy(out=c2[:], in_=cos_sb[:].unsqueeze(3).to_broadcast([P, 2, HD // 2, 2]))
+        nc.scalar.copy(out=s2[:, :, :, 0:1], in_=sin_sb[:].unsqueeze(3))
+        nc.scalar.mul(out=s2[:, :, :, 1:2], in_=sin_sb[:].unsqueeze(3), mul=-1.0)
         cs = const.tile([P, 2, 2, 4, HD], F32, name="cs")
         for e in range(2):
             for f, table in enumerate((c2, s2)):
-                nc.gpsimd.tensor_scalar(
+                nc.scalar.copy(
                     out=cs[:, e, f, :, :],
-                    in0=table[:, e, :, :].rearrange("p i z -> p (i z)").unsqueeze(1).to_broadcast([P, 4, HD]),
-                    scalar1=1.0,
-                    scalar2=0.0,
-                    op0=MULT,
-                    op1=ADD,
+                    in_=table[:, e, :, :].rearrange("p i z -> p (i z)").unsqueeze(1).to_broadcast([P, 4, HD]),
                 )
         xc = const.tile([P, TOKEN_TILES, 512], U32, name="xc", align_bytes=64)
         xs = const.tile([P, TOKEN_TILES, 512], U8, name="xs", align_bytes=64)
 
-        def w_rows(c, g, lo, hi):
+        def load_weights(c, g, lo, hi):
+            if lo == 0:
+                raw = wraw.tile([P, 4, CHUNK], BF16, name="raw")
+                raw_tiles[(c, g)] = raw
             w, j = c // 2, c % 2
-            return weights[w][512 * g : 512 * (g + 1), CHUNK * j + lo : CHUNK * j + hi].rearrange(
-                "(p t) c -> p t c", t=4
+            nc.sync.dma_start(
+                out=raw_tiles[(c, g)][:, :, lo:hi],
+                in_=weights[w][512 * g : 512 * (g + 1), CHUNK * j + lo : CHUNK * j + hi].rearrange(
+                    "(p t) c -> p t c", t=4
+                ),
             )
-
-        def load_unit(c, g):
-            raw = wraw.tile([P, 4, CHUNK], BF16, name="raw")
-            raw_tiles[(c, g)] = raw
-            nc.sync.dma_start(out=raw[:], in_=w_rows(c, g, 0, CHUNK))
 
         def load_x(b):
             x_sb = xraw.tile([P, 2, D], BF16, name="x_sb")
             nc.sync.dma_start(out=x_sb[:], in_=x[b].rearrange("(p e) k -> p e k", e=2))
             x_tiles[b] = x_sb
 
-        def prep_x(b, e):
-            m = 2 * b + e
+        def x_transposes(b, e):
             words = x_tiles[b][:, e, :].bitcast(F32)
-            xg = xgrp.tile([P, D], BF16, name="xg", align_bytes=64)
-            xg_words = xg[:].bitcast(F32)
             for gp in range(2):
                 bank = accp.tile([P, 2, 2, P], F32, name="bank", tag="acc")
+                xbank_tiles[(b, e, gp)] = bank
                 for gg in range(2):
                     g = 2 * gp + gg
                     for u in range(2):
                         nc.tensor.transpose(bank[:, gg, u, :], words[:, 256 * g + u : 256 * (g + 1) : 2], ident[:])
+
+        def x_copies(b, e):
+            xg = xgrp.tile([P, D], BF16, name="xg", align_bytes=64)
+            xg_tiles[(b, e)] = xg
+            xg_words = xg[:].bitcast(F32)
+            for gp in range(2):
                 nc.vector.tensor_copy(
                     out=xg_words[:, 512 * gp : 512 * (gp + 1)].rearrange("p (g r u) -> p g r u", g=2, u=2),
-                    in_=bank[:].rearrange("p g u r -> p g r u"),
+                    in_=xbank_tiles[(b, e, gp)][:].rearrange("p g u r -> p g r u"),
                 )
-            nc.vector.quantize_mx(out=xc[:, m, :].bitcast(FP8X4), scales=xs[:, m, :], in_=xg[:])
+
+        def x_quantise(b, e):
+            m = 2 * b + e
+            nc.vector.quantize_mx(out=xc[:, m, :].bitcast(FP8X4), scales=xs[:, m, :], in_=xg_tiles[(b, e)][:])
 
         def unit_src(unit, a):
             k, gp = unit // 2, unit % 2
@@ -134,11 +133,10 @@ def tile_llamaattention_pa_kernel(tc, x, Wq, Wk, rope_cos, rope_sin, out_0, out_
                 pt = ptp.tile([P, 256, 4], BF16, name="pt", tag="pt")
                 pt_tiles[(unit, a)] = pt
                 for c1 in range(0, PE_COLS[a], P):
-                    c_end = min(c1 + P, PE_COLS[a])
                     nc.tensor.matmul(
-                        out=pt[:, c1:c_end, :].rearrange("p c t -> p t c"),
+                        out=pt[:, c1 : c1 + P, :].rearrange("p c t -> p t c"),
                         lhsT=ident_bf[:],
-                        rhs=src[:, :, c1:c_end],
+                        rhs=src[:, :, c1 : c1 + P],
                         start=True,
                         stop=True,
                     )
@@ -151,11 +149,11 @@ def tile_llamaattention_pa_kernel(tc, x, Wq, Wk, rope_cos, rope_sin, out_0, out_
                 s_end = HALF - v_cols
                 src = unit_src(unit, a)
                 dst = grp[:, a, :, :]
+                if v_cols:
+                    nc.vector.tensor_copy(out=dst[:, s_end:, :], in_=src[:, :, s_end:].rearrange("p t c -> p c t"))
                 nc.scalar.copy(
                     out=dst[:, PE_COLS[a] : s_end, :], in_=src[:, :, PE_COLS[a] : s_end].rearrange("p t c -> p c t")
                 )
-                if v_cols:
-                    nc.vector.tensor_copy(out=dst[:, s_end:, :], in_=src[:, :, s_end:].rearrange("p t c -> p c t"))
 
         def empty_pass_through(unit):
             k, gp = unit // 2, unit % 2
@@ -163,8 +161,8 @@ def tile_llamaattention_pa_kernel(tc, x, Wq, Wk, rope_cos, rope_sin, out_0, out_
             nc.scalar.copy(out=grp_tiles[unit][:, 0, : PE_COLS[0], :], in_=pt_tiles[(unit, 0)][:, : PE_COLS[0], :])
             nc.vector.tensor_copy(out=grp_tiles[unit][:, 1, : PE_COLS[1], :], in_=pt_tiles[(unit, 1)][:, : PE_COLS[1], :])
             if n == 1 and c + 2 < N_CHUNKS:
-                load_unit(c + 2, 2 * gp)
-                load_unit(c + 2, 2 * gp + 1)
+                load_weights(c + 2, 2 * gp, 0, CHUNK)
+                load_weights(c + 2, 2 * gp + 1, 0, CHUNK)
 
         def quantise(unit):
             k, gp = unit // 2, unit % 2
@@ -179,76 +177,67 @@ def tile_llamaattention_pa_kernel(tc, x, Wq, Wk, rope_cos, rope_sin, out_0, out_
                 in_=grp_tiles[unit][:].rearrange("p a c t -> p (a c t)"),
             )
 
-        def matmuls(bank):
-            k, m = bank // TOKEN_TILES, bank % TOKEN_TILES
+        def matmuls(pair):
+            k, b = pair // B, pair % B
             wc, ws = code_tiles[k]
-            acc = accp.tile([P, 512], F32, name="acc", tag="acc")
-            acc_tiles[bank] = acc
-            for g in range(PASSES):
-                nc.tensor.matmul_mx(
-                    out=acc[:],
-                    lhsT=xc[:, m, P * g : P * (g + 1)].bitcast(FP8X4),
-                    lhsT_scale=xs[:, m, P * g : P * (g + 1)],
-                    rhs=wc[:, g, :].bitcast(FP8X4),
-                    rhs_scale=ws[:, g, :],
-                    start=(g == 0),
-                    stop=(g == PASSES - 1),
-                )
+            for e in range(2):
+                m = 2 * b + e
+                acc = accp.tile([P, 512], F32, name="acc", tag="acc")
+                acc_tiles[(pair, e)] = acc
+                for g in range(PASSES):
+                    nc.tensor.matmul_mx(
+                        out=acc[:],
+                        lhsT=xc[:, m, P * g : P * (g + 1)].bitcast(FP8X4),
+                        lhsT_scale=xs[:, m, P * g : P * (g + 1)],
+                        rhs=wc[:, g, :].bitcast(FP8X4),
+                        rhs_scale=ws[:, g, :],
+                        start=(g == 0),
+                        stop=(g == PASSES - 1),
+                    )
 
-        def rotate(bank):
-            k, m = bank // TOKEN_TILES, bank % TOKEN_TILES
+        def rotate(pair):
+            k, b = pair // B, pair % B
             c, n = groups[k]
-            b, e = m // 2, m % 2
-            if e == 0:
-                uw_new = ep.tile([P, 2, 4, 2, HD], F32, name="uw")
-                uw_tiles[b] = uw_new
-                r_new = rp.tile([P, 4, 2, HD], F32, name="r_t")
-                r_tiles[b] = r_new
-            uw = uw_tiles[b]
-            r_t = r_tiles[b]
-            nc.vector.tensor_tensor(
-                out=uw[:, :, :, e, :],
-                in0=acc_tiles[bank][:].rearrange("p (h d) -> p h d", h=4).unsqueeze(1).to_broadcast([P, 2, 4, HD]),
-                in1=cs[:, e, :, :, :],
-                op=MULT,
+            uw = ep.tile([P, 2, 4, 2, HD], F32, name="uw")
+            r_t = rp.tile([P, 4, 2, HD], F32, name="r_t")
+            for e in range(2):
+                nc.vector.tensor_tensor(
+                    out=uw[:, :, :, e, :],
+                    in0=acc_tiles[(pair, e)][:]
+                    .rearrange("p (h d) -> p h d", h=4)
+                    .unsqueeze(1)
+                    .to_broadcast([P, 2, 4, HD]),
+                    in1=cs[:, e, :, :, :],
+                    op=MULT,
+                )
+            adder = nc.vector if pair == n_pairs - 1 else nc.gpsimd
+            adder.tensor_tensor(
+                out=r_t[:].rearrange("p h e (i z) -> p (h e i) z", z=2),
+                in0=uw[:, 0, :, :, :].rearrange("p h e (i z) -> p (h e i) z", z=2),
+                in1=uw[:, 1, :, :, :].rearrange("p h e (i z) -> p (h e i) z", z=2)[:, :, ::-1],
+                op=ADD,
             )
-            if k == len(groups) - 1 and b == B - 1:
-                adder = nc.vector if e == 1 else nc.gpsimd
-                adder.tensor_tensor(
-                    out=r_t[:, :, e, :].rearrange("p h (i z) -> p h i z", z=2),
-                    in0=uw[:, 0, :, e, :].rearrange("p h (i z) -> p h i z", z=2),
-                    in1=uw[:, 1, :, e, :].rearrange("p h (i z) -> p h i z", z=2)[:, :, :, ::-1],
-                    op=ADD,
-                )
-            elif e == 1:
-                nc.gpsimd.tensor_tensor(
-                    out=r_t[:].rearrange("p h e (i z) -> p (h e i) z", z=2),
-                    in0=uw[:, 0, :, :, :].rearrange("p h e (i z) -> p (h e i) z", z=2),
-                    in1=uw[:, 1, :, :, :].rearrange("p h e (i z) -> p (h e i) z", z=2)[:, :, ::-1],
-                    op=ADD,
-                )
-            if e == 1:
-                h0 = ((c % 2) * CHUNK + HALF * n) // HD
-                nc.sync.dma_start(
-                    out=outs[c // 2][b, h0 : h0 + 4, :, :].rearrange("h (p e) d -> p h (e d)", e=2),
-                    in_=r_t[:].rearrange("p h e d -> p h (e d)"),
-                )
+            h0 = ((c % 2) * CHUNK + HALF * n) // HD
+            nc.sync.dma_start(
+                out=outs[c // 2][b, h0 : h0 + 4, :, :].rearrange("h (p e) d -> p h (e d)", e=2),
+                in_=r_t[:].rearrange("p h e d -> p h (e d)"),
+            )
 
         with tc.manual_schedule():
             load_x(0)
             load_x(1)
-            for g in range(PASSES):
-                raw = wraw.tile([P, 4, CHUNK], BF16, name="raw")
-                raw_tiles[(0, g)] = raw
-                nc.sync.dma_start(out=raw[:, :, :HALF], in_=w_rows(0, g, 0, HALF))
-            for g in range(PASSES):
-                nc.sync.dma_start(out=raw_tiles[(0, g)][:, :, HALF:], in_=w_rows(0, g, HALF, CHUNK))
-            for g in range(PASSES):
-                load_unit(1, g)
-            for m in range(TOKEN_TILES):
-                prep_x(m // 2, m % 2)
+            for c in range(CHUNKS_IN_HALVES):
+                for lo in (0, HALF):
+                    for g in range(PASSES):
+                        load_weights(c, g, lo, lo + HALF)
+            for b in range(B):
+                for e in range(2):
+                    x_transposes(b, e)
+                for e in range(2):
+                    x_copies(b, e)
+                for e in range(2):
+                    x_quantise(b, e)
             pass_through(0)
-            n_pairs = n_banks // 2
             for step in range(n_units + LAG):
                 if step < n_units:
                     direct_copies(step)
@@ -256,13 +245,11 @@ def tile_llamaattention_pa_kernel(tc, x, Wq, Wk, rope_cos, rope_sin, out_0, out_
                 if step + 1 < n_units:
                     pass_through(step + 1)
                 pair = step - LAG
+                if 1 <= pair + 1 < n_pairs:
+                    matmuls(pair + 1)
                 if pair >= 0:
-                    rotate(2 * pair)
-                    rotate(2 * pair + 1)
+                    rotate(pair)
                 if step < n_units:
                     quantise(step)
-                nxt = pair + 1
-                if 0 <= nxt < n_pairs:
-                    assert 2 * (nxt // 2) + 1 <= step
-                    matmuls(2 * nxt)
-                    matmuls(2 * nxt + 1)
+                if step == 1:
+                    matmuls(0)

@@ -20,7 +20,7 @@ HALF = 512
 N_CHUNKS = 2 * E // CHUNK
 TOKEN_TILES = B * S // P
 
-PE_COLS = (256, 128)
+PE_COLS = (224, 128)
 HEAD_VECTOR_COLS = ((0, 128), (0, 128))
 RAW_BUFS = 8
 CHUNKS_IN_HALVES = 2
@@ -133,10 +133,11 @@ def tile_llamaattention_pa_kernel(tc, x, Wq, Wk, rope_cos, rope_sin, out_0, out_
                 pt = ptp.tile([P, 256, 4], BF16, name="pt", tag="pt")
                 pt_tiles[(unit, a)] = pt
                 for c1 in range(0, PE_COLS[a], P):
+                    c_end = min(c1 + P, PE_COLS[a])
                     nc.tensor.matmul(
-                        out=pt[:, c1 : c1 + P, :].rearrange("p c t -> p t c"),
+                        out=pt[:, c1:c_end, :].rearrange("p c t -> p t c"),
                         lhsT=ident_bf[:],
-                        rhs=src[:, :, c1 : c1 + P],
+                        rhs=src[:, :, c1:c_end],
                         start=True,
                         stop=True,
                     )

@@ -20,8 +20,10 @@ HALF = 512
 N_CHUNKS = 2 * E // CHUNK
 TOKEN_TILES = B * S // P
 
-PE_COLS = (224, 128)
-HEAD_VECTOR_COLS = ((0, 128), (0, 128))
+PE_COLS = (160, 160)
+HEAD_UNITS = 3
+HEAD_PE_COLS = (256, 160)
+HEAD_VECTOR_COLS = (192, 160)
 RAW_BUFS = 8
 CHUNKS_IN_HALVES = 2
 LAG = 3
@@ -66,18 +68,13 @@ def tile_llamaattention_pa_kernel(tc, x, Wq, Wk, rope_cos, rope_sin, out_0, out_
         make_identity(nc, ident[:])
         ident_bf = const.tile([P, P], BF16, name="ident_bf")
         make_identity(nc, ident_bf[:])
-        c2 = const.tile([P, 2, HD // 2, 2], F32, name="c2")
-        s2 = const.tile([P, 2, HD // 2, 2], F32, name="s2")
-        nc.scalar.copy(out=c2[:], in_=cos_sb[:].unsqueeze(3).to_broadcast([P, 2, HD // 2, 2]))
-        nc.scalar.copy(out=s2[:, :, :, 0:1], in_=sin_sb[:].unsqueeze(3))
-        nc.scalar.mul(out=s2[:, :, :, 1:2], in_=sin_sb[:].unsqueeze(3), mul=-1.0)
-        cs = const.tile([P, 2, 2, 4, HD], F32, name="cs")
-        for e in range(2):
-            for f, table in enumerate((c2, s2)):
-                nc.scalar.copy(
-                    out=cs[:, e, f, :, :],
-                    in_=table[:, e, :, :].rearrange("p i z -> p (i z)").unsqueeze(1).to_broadcast([P, 4, HD]),
-                )
+        cs = const.tile([P, 2, 2, HD // 2, 2], F32, name="cs")
+        for out, table, factor in (
+            (cs[:, :, 0, :, :], cos_sb[:].unsqueeze(3).to_broadcast([P, 2, HD // 2, 2]), 1.0),
+            (cs[:, :, 1, :, 0:1], sin_sb[:].unsqueeze(3), 1.0),
+            (cs[:, :, 1, :, 1:2], sin_sb[:].unsqueeze(3), -1.0),
+        ):
+            nc.gpsimd.tensor_scalar(out=out, in0=table, scalar1=factor, scalar2=0.0, op0=MULT, op1=ADD)
         xc = const.tile([P, TOKEN_TILES, 512], U32, name="xc", align_bytes=64)
         xs = const.tile([P, TOKEN_TILES, 512], U8, name="xs", align_bytes=64)
 
@@ -113,7 +110,8 @@ def tile_llamaattention_pa_kernel(tc, x, Wq, Wk, rope_cos, rope_sin, out_0, out_
             xg_tiles[(b, e)] = xg
             xg_words = xg[:].bitcast(F32)
             for gp in range(2):
-                nc.vector.tensor_copy(
+                copy = (nc.vector.tensor_copy, nc.scalar.copy)[gp]
+                copy(
                     out=xg_words[:, 512 * gp : 512 * (gp + 1)].rearrange("p (g r u) -> p g r u", g=2, u=2),
                     in_=xbank_tiles[(b, e, gp)][:].rearrange("p g u r -> p g r u"),
                 )
@@ -127,13 +125,17 @@ def tile_llamaattention_pa_kernel(tc, x, Wq, Wk, rope_cos, rope_sin, out_0, out_
             c, n = groups[k]
             return raw_tiles[(c, 2 * gp + a)][:, :, HALF * n : HALF * (n + 1)]
 
+        def pe_cols(unit, a):
+            return (HEAD_PE_COLS if unit < HEAD_UNITS else PE_COLS)[a]
+
         def pass_through(unit):
             for a in range(2):
                 src = unit_src(unit, a)
                 pt = ptp.tile([P, 256, 4], BF16, name="pt", tag="pt")
                 pt_tiles[(unit, a)] = pt
-                for c1 in range(0, PE_COLS[a], P):
-                    c_end = min(c1 + P, PE_COLS[a])
+                n_pe = pe_cols(unit, a)
+                for c1 in range(0, n_pe, P):
+                    c_end = min(c1 + P, n_pe)
                     nc.tensor.matmul(
                         out=pt[:, c1:c_end, :].rearrange("p c t -> p t c"),
                         lhsT=ident_bf[:],
@@ -146,21 +148,22 @@ def tile_llamaattention_pa_kernel(tc, x, Wq, Wk, rope_cos, rope_sin, out_0, out_
             grp = wgrp.tile([P, 2, HALF, 4], BF16, name="grp", align_bytes=64)
             grp_tiles[unit] = grp
             for a in range(2):
-                v_cols = HEAD_VECTOR_COLS[unit][a] if unit < len(HEAD_VECTOR_COLS) else 0
+                v_cols = HEAD_VECTOR_COLS[a] if unit < HEAD_UNITS else 0
+                n_pe = pe_cols(unit, a)
                 s_end = HALF - v_cols
                 src = unit_src(unit, a)
                 dst = grp[:, a, :, :]
                 if v_cols:
                     nc.vector.tensor_copy(out=dst[:, s_end:, :], in_=src[:, :, s_end:].rearrange("p t c -> p c t"))
-                nc.scalar.copy(
-                    out=dst[:, PE_COLS[a] : s_end, :], in_=src[:, :, PE_COLS[a] : s_end].rearrange("p t c -> p c t")
-                )
+                nc.scalar.copy(out=dst[:, n_pe:s_end, :], in_=src[:, :, n_pe:s_end].rearrange("p t c -> p c t"))
 
         def empty_pass_through(unit):
             k, gp = unit // 2, unit % 2
             c, n = groups[k]
-            nc.scalar.copy(out=grp_tiles[unit][:, 0, : PE_COLS[0], :], in_=pt_tiles[(unit, 0)][:, : PE_COLS[0], :])
-            nc.vector.tensor_copy(out=grp_tiles[unit][:, 1, : PE_COLS[1], :], in_=pt_tiles[(unit, 1)][:, : PE_COLS[1], :])
+            for a in range(2):
+                copy = nc.vector.tensor_copy if a == 0 and unit >= HEAD_UNITS else nc.scalar.copy
+                n_pe = pe_cols(unit, a)
+                copy(out=grp_tiles[unit][:, a, :n_pe, :], in_=pt_tiles[(unit, a)][:, :n_pe, :])
             if n == 1 and c + 2 < N_CHUNKS:
                 load_weights(c + 2, 2 * gp, 0, CHUNK)
                 load_weights(c + 2, 2 * gp + 1, 0, CHUNK)
@@ -208,7 +211,10 @@ def tile_llamaattention_pa_kernel(tc, x, Wq, Wk, rope_cos, rope_sin, out_0, out_
                     .rearrange("p (h d) -> p h d", h=4)
                     .unsqueeze(1)
                     .to_broadcast([P, 2, 4, HD]),
-                    in1=cs[:, e, :, :, :],
+                    in1=cs[:, e, :, :, :]
+                    .rearrange("p f i z -> p f (i z)")
+                    .unsqueeze(2)
+                    .to_broadcast([P, 2, 4, HD]),
                     op=MULT,
                 )
             adder = nc.vector if pair == n_pairs - 1 else nc.gpsimd
@@ -240,14 +246,17 @@ def tile_llamaattention_pa_kernel(tc, x, Wq, Wk, rope_cos, rope_sin, out_0, out_
                     x_quantise(b, e)
             pass_through(0)
             for step in range(n_units + LAG):
+                pair = step - LAG
                 if step < n_units:
                     direct_copies(step)
                     empty_pass_through(step)
+                if 1 <= pair + 1 < n_pairs:
+                    if pair == 1:
+                        matmuls(pair)
+                    if pair != 0:
+                        matmuls(pair + 1)
                 if step + 1 < n_units:
                     pass_through(step + 1)
-                pair = step - LAG
-                if 1 <= pair + 1 < n_pairs:
-                    matmuls(pair + 1)
                 if pair >= 0:
                     rotate(pair)
                 if step < n_units:

@@ -20,7 +20,7 @@ HALF = 512
 N_CHUNKS = 2 * E // CHUNK
 TOKEN_TILES = B * S // P
 
-PE_COLS = (160, 160)
+PE_COLS = (160, 96)
 HEAD_UNITS = 3
 HEAD_PE_COLS = (256, 160)
 HEAD_VECTOR_COLS = (192, 160)
@@ -155,13 +155,16 @@ def tile_llamaattention_pa_kernel(tc, x, Wq, Wk, rope_cos, rope_sin, out_0, out_
                 dst = grp[:, a, :, :]
                 if v_cols:
                     nc.vector.tensor_copy(out=dst[:, s_end:, :], in_=src[:, :, s_end:].rearrange("p t c -> p c t"))
-                nc.scalar.copy(out=dst[:, n_pe:s_end, :], in_=src[:, :, n_pe:s_end].rearrange("p t c -> p c t"))
+                nc.scalar.copy(
+                    out=dst[:, n_pe:s_end, :].rearrange("p (b c) (h t) -> p b h c t", c=8, h=2),
+                    in_=src[:, :, n_pe:s_end].rearrange("p (h t) (b c) -> p b h c t", c=8, h=2),
+                )
 
         def empty_pass_through(unit):
             k, gp = unit // 2, unit % 2
             c, n = groups[k]
             for a in range(2):
-                copy = nc.vector.tensor_copy if a == 0 and unit >= HEAD_UNITS else nc.scalar.copy
+                copy = nc.vector.tensor_copy if a == 1 and unit >= HEAD_UNITS else nc.scalar.copy
                 n_pe = pe_cols(unit, a)
                 copy(out=grp_tiles[unit][:, a, :n_pe, :], in_=pt_tiles[(unit, a)][:, :n_pe, :])
             if n == 1 and c + 2 < N_CHUNKS:

@@ -20,10 +20,11 @@ HALF = 512
 N_CHUNKS = 2 * E // CHUNK
 TOKEN_TILES = B * S // P
 
-PE_COLS = (160, 96)
-HEAD_UNITS = 3
-HEAD_PE_COLS = (256, 160)
-HEAD_VECTOR_COLS = (192, 160)
+PE_COLS = (192, 64)
+HEAD_UNITS = 2
+HEAD_PE_COLS = (256, 224)
+VECTOR_UNITS = 4
+VECTOR_COLS = (64, 256)
 RAW_BUFS = 8
 CHUNKS_IN_HALVES = 2
 LAG = 3
@@ -41,7 +42,7 @@ def tile_llamaattention_pa_kernel(tc, x, Wq, Wk, rope_cos, rope_sin, out_0, out_
         xraw = ctx.enter_context(tc.tile_pool(name="xraw", bufs=2))
         xgrp = ctx.enter_context(tc.tile_pool(name="xgrp", bufs=2))
         wraw = ctx.enter_context(tc.tile_pool(name="wraw", bufs=RAW_BUFS))
-        wgrp = ctx.enter_context(tc.tile_pool(name="wgrp", bufs=3))
+        wgrp = ctx.enter_context(tc.tile_pool(name="wgrp", bufs=4))
         wcode = ctx.enter_context(tc.tile_pool(name="wcode", bufs=4))
         ep = ctx.enter_context(tc.tile_pool(name="ep", bufs=3))
         rp = ctx.enter_context(tc.tile_pool(name="rp", bufs=5))
@@ -144,21 +145,23 @@ def tile_llamaattention_pa_kernel(tc, x, Wq, Wk, rope_cos, rope_sin, out_0, out_
                         stop=True,
                     )
 
+        def by_lines(dst):
+            return dst.rearrange("p (b c) (h t) -> p b h c t", c=8, h=2)
+
+        def rows_by_lines(src):
+            return src.rearrange("p (h t) (b c) -> p b h c t", c=8, h=2)
+
         def direct_copies(unit):
             grp = wgrp.tile([P, 2, HALF, 4], BF16, name="grp", align_bytes=64)
             grp_tiles[unit] = grp
             for a in range(2):
-                v_cols = HEAD_VECTOR_COLS[a] if unit < HEAD_UNITS else 0
+                v_cols = VECTOR_COLS[a] if unit < VECTOR_UNITS else 0
                 n_pe = pe_cols(unit, a)
                 s_end = HALF - v_cols
                 src = unit_src(unit, a)
-                dst = grp[:, a, :, :]
                 if v_cols:
-                    nc.vector.tensor_copy(out=dst[:, s_end:, :], in_=src[:, :, s_end:].rearrange("p t c -> p c t"))
-                nc.scalar.copy(
-                    out=dst[:, n_pe:s_end, :].rearrange("p (b c) (h t) -> p b h c t", c=8, h=2),
-                    in_=src[:, :, n_pe:s_end].rearrange("p (h t) (b c) -> p b h c t", c=8, h=2),
-                )
+                    nc.vector.tensor_copy(out=by_lines(grp[:, a, s_end:, :]), in_=rows_by_lines(src[:, :, s_end:]))
+                nc.scalar.copy(out=by_lines(grp[:, a, n_pe:s_end, :]), in_=rows_by_lines(src[:, :, n_pe:s_end]))
 
         def empty_pass_through(unit):
             k, gp = unit // 2, unit % 2
@@ -253,13 +256,12 @@ def tile_llamaattention_pa_kernel(tc, x, Wq, Wk, rope_cos, rope_sin, out_0, out_
                 if step < n_units:
                     direct_copies(step)
                     empty_pass_through(step)
-                if 1 <= pair + 1 < n_pairs:
-                    if pair == 1:
-                        matmuls(pair)
-                    if pair != 0:
-                        matmuls(pair + 1)
                 if step + 1 < n_units:
                     pass_through(step + 1)
+                if step == 2:
+                    matmuls(1)
+                if 2 <= pair + 1 < n_pairs:
+                    matmuls(pair + 1)
                 if pair >= 0:
                     rotate(pair)
                 if step < n_units:

@@ -57,6 +57,7 @@ def tile_llamaattention_pa_kernel(tc, x, Wq, Wk, rope_cos, rope_sin, out_0, out_
         grp_tiles = {}
         pt_tiles = {}
         acc_tiles = {}
+        pair_tiles = {}
         groups = [(c, n) for c in range(N_CHUNKS) for n in range(2)]
         n_units = 2 * len(groups)
         n_pairs = B * len(groups)
@@ -205,11 +206,10 @@ def tile_llamaattention_pa_kernel(tc, x, Wq, Wk, rope_cos, rope_sin, out_0, out_
                         stop=(g == PASSES - 1),
                     )
 
-        def rotate(pair):
-            k, b = pair // B, pair % B
-            c, n = groups[k]
+        def products(pair):
             uw = ep.tile([P, 2, 4, 2, HD], F32, name="uw")
             r_t = rp.tile([P, 4, 2, HD], F32, name="r_t")
+            pair_tiles[pair] = (uw, r_t)
             for e in range(2):
                 nc.vector.tensor_tensor(
                     out=uw[:, :, :, e, :],
@@ -223,18 +223,33 @@ def tile_llamaattention_pa_kernel(tc, x, Wq, Wk, rope_cos, rope_sin, out_0, out_
                     .to_broadcast([P, 2, 4, HD]),
                     op=MULT,
                 )
-            adder = nc.vector if pair == n_pairs - 1 else nc.gpsimd
-            adder.tensor_tensor(
-                out=r_t[:].rearrange("p h e (i z) -> p (h e i) z", z=2),
-                in0=uw[:, 0, :, :, :].rearrange("p h e (i z) -> p (h e i) z", z=2),
-                in1=uw[:, 1, :, :, :].rearrange("p h e (i z) -> p (h e i) z", z=2)[:, :, ::-1],
+
+        def add_and_store(engine, pair, lo, hi):
+            k, b = pair // B, pair % B
+            c, n = groups[k]
+            uw, r_t = pair_tiles[pair]
+            engine.tensor_tensor(
+                out=r_t[:, lo:hi, :, :].rearrange("p h e (i z) -> p (h e i) z", z=2),
+                in0=uw[:, 0, lo:hi, :, :].rearrange("p h e (i z) -> p (h e i) z", z=2),
+                in1=uw[:, 1, lo:hi, :, :].rearrange("p h e (i z) -> p (h e i) z", z=2)[:, :, ::-1],
                 op=ADD,
             )
             h0 = ((c % 2) * CHUNK + HALF * n) // HD
             nc.sync.dma_start(
-                out=outs[c // 2][b, h0 : h0 + 4, :, :].rearrange("h (p e) d -> p h (e d)", e=2),
-                in_=r_t[:].rearrange("p h e d -> p h (e d)"),
+                out=outs[c // 2][b, h0 + lo : h0 + hi, :, :].rearrange("h (p e) d -> p h (e d)", e=2),
+                in_=r_t[:, lo:hi, :, :].rearrange("p h e d -> p h (e d)"),
             )
+
+        def rotate(pair):
+            products(pair)
+            if pair < n_pairs - 2:
+                add_and_store(nc.gpsimd, pair, 0, 4)
+            elif pair == n_pairs - 2:
+                add_and_store(nc.gpsimd, pair, 0, 2)
+            else:
+                add_and_store(nc.vector, pair - 1, 2, 4)
+                for lo in (0, 2):
+                    add_and_store(nc.vector, pair, lo, lo + 2)
 
         with tc.manual_schedule():
             load_x(0)

from contextlib import ExitStack

import concourse.mybir as mybir
from concourse.masks import make_identity

F32 = mybir.dt.float32
BF16 = mybir.dt.bfloat16
U32 = mybir.dt.uint32
U8 = mybir.dt.uint8
FP8X4 = mybir.dt.float8_e5m2_x4
MULT = mybir.AluOpType.mult
ADD = mybir.AluOpType.add

B, S, D, H, HD = 2, 256, 2048, 16, 128
E = H * HD
P = 128
PASSES = D // 512
CHUNK = 1024
HALF = 512
N_CHUNKS = 2 * E // CHUNK
TOKEN_TILES = B * S // P

PE_COLS = (192, 64)
HEAD_UNITS = 2
HEAD_PE_COLS = (256, 224)
VECTOR_UNITS = 4
VECTOR_COLS = (64, 256)
RAW_BUFS = 8
CHUNKS_IN_HALVES = 2
LAG = 3

FLOPS = 2 * B * S * D * 2 * E


def tile_llamaattention_pa_kernel(tc, x, Wq, Wk, rope_cos, rope_sin, out_0, out_1):
    nc = tc.nc
    weights = (Wq, Wk)
    outs = (out_0, out_1)

    with ExitStack() as ctx:
        const = ctx.enter_context(tc.tile_pool(name="const", bufs=1))
        xraw = ctx.enter_context(tc.tile_pool(name="xraw", bufs=2))
        xgrp = ctx.enter_context(tc.tile_pool(name="xgrp", bufs=2))
        wraw = ctx.enter_context(tc.tile_pool(name="wraw", bufs=RAW_BUFS))
        wgrp = ctx.enter_context(tc.tile_pool(name="wgrp", bufs=4))
        wcode = ctx.enter_context(tc.tile_pool(name="wcode", bufs=4))
        ep = ctx.enter_context(tc.tile_pool(name="ep", bufs=3))
        rp = ctx.enter_context(tc.tile_pool(name="rp", bufs=5))
        accp = ctx.enter_context(tc.psum_pool(name="accp", bufs=4))
        ptp = ctx.enter_context(tc.psum_pool(name="ptp", bufs=4))

        raw_tiles = {}
        x_tiles = {}
        xbank_tiles = {}
        xg_tiles = {}
        code_tiles = {}
        grp_tiles = {}
        pt_tiles = {}
        acc_tiles = {}
        pair_tiles = {}
        groups = [(c, n) for c in range(N_CHUNKS) for n in range(2)]
        n_units = 2 * len(groups)
        n_pairs = B * len(groups)

        cos_sb = const.tile([P, 2, HD // 2], BF16, name="cos_sb")
        sin_sb = const.tile([P, 2, HD // 2], BF16, name="sin_sb")
        nc.scalar.dma_start(out=cos_sb[:], in_=rope_cos.rearrange("(p e) i -> p e i", e=2))
        nc.scalar.dma_start(out=sin_sb[:], in_=rope_sin.rearrange("(p e) i -> p e i", e=2))
        ident = const.tile([P, P], F32, name="ident")
        make_identity(nc, ident[:])
        ident_bf = const.tile([P, P], BF16, name="ident_bf")
        make_identity(nc, ident_bf[:])
        cs = const.tile([P, 2, 2, HD // 2, 2], F32, name="cs")
        for out, table, factor in (
            (cs[:, :, 0, :, :], cos_sb[:].unsqueeze(3).to_broadcast([P, 2, HD // 2, 2]), 1.0),
            (cs[:, :, 1, :, 0:1], sin_sb[:].unsqueeze(3), 1.0),
            (cs[:, :, 1, :, 1:2], sin_sb[:].unsqueeze(3), -1.0),
        ):
            nc.gpsimd.tensor_scalar(out=out, in0=table, scalar1=factor, scalar2=0.0, op0=MULT, op1=ADD)
        xc = const.tile([P, TOKEN_TILES, 512], U32, name="xc", align_bytes=64)
        xs = const.tile([P, TOKEN_TILES, 512], U8, name="xs", align_bytes=64)

        def load_weights(c, g, lo, hi):
            if lo == 0:
                raw = wraw.tile([P, 4, CHUNK], BF16, name="raw")
                raw_tiles[(c, g)] = raw
            w, j = c // 2, c % 2
            nc.sync.dma_start(
                out=raw_tiles[(c, g)][:, :, lo:hi],
                in_=weights[w][512 * g : 512 * (g + 1), CHUNK * j + lo : CHUNK * j + hi].rearrange(
                    "(p t) c -> p t c", t=4
                ),
            )

        def load_x(b):
            x_sb = xraw.tile([P, 2, D], BF16, name="x_sb")
            nc.sync.dma_start(out=x_sb[:], in_=x[b].rearrange("(p e) k -> p e k", e=2))
            x_tiles[b] = x_sb

        def x_transposes(b, e):
            words = x_tiles[b][:, e, :].bitcast(F32)
            for gp in range(2):
                bank = accp.tile([P, 2, 2, P], F32, name="bank", tag="acc")
                xbank_tiles[(b, e, gp)] = bank
                for gg in range(2):
                    g = 2 * gp + gg
                    for u in range(2):
                        nc.tensor.transpose(bank[:, gg, u, :], words[:, 256 * g + u : 256 * (g + 1) : 2], ident[:])

        def x_copies(b, e):
            xg = xgrp.tile([P, D], BF16, name="xg", align_bytes=64)
            xg_tiles[(b, e)] = xg
            xg_words = xg[:].bitcast(F32)
            for gp in range(2):
                copy = (nc.vector.tensor_copy, nc.scalar.copy)[gp]
                copy(
                    out=xg_words[:, 512 * gp : 512 * (gp + 1)].rearrange("p (g r u) -> p g r u", g=2, u=2),
                    in_=xbank_tiles[(b, e, gp)][:].rearrange("p g u r -> p g r u"),
                )

        def x_quantise(b, e):
            m = 2 * b + e
            nc.vector.quantize_mx(out=xc[:, m, :].bitcast(FP8X4), scales=xs[:, m, :], in_=xg_tiles[(b, e)][:])

        def unit_src(unit, a):
            k, gp = unit // 2, unit % 2
            c, n = groups[k]
            return raw_tiles[(c, 2 * gp + a)][:, :, HALF * n : HALF * (n + 1)]

        def pe_cols(unit, a):
            return (HEAD_PE_COLS if unit < HEAD_UNITS else PE_COLS)[a]

        def pass_through(unit):
            for a in range(2):
                src = unit_src(unit, a)
                pt = ptp.tile([P, 256, 4], BF16, name="pt", tag="pt")
                pt_tiles[(unit, a)] = pt
                n_pe = pe_cols(unit, a)
                for c1 in range(0, n_pe, P):
                    c_end = min(c1 + P, n_pe)
                    nc.tensor.matmul(
                        out=pt[:, c1:c_end, :].rearrange("p c t -> p t c"),
                        lhsT=ident_bf[:],
                        rhs=src[:, :, c1:c_end],
                        start=True,
                        stop=True,
                    )

        def by_lines(dst):
            return dst.rearrange("p (b c) (h t) -> p b h c t", c=8, h=2)

        def rows_by_lines(src):
            return src.rearrange("p (h t) (b c) -> p b h c t", c=8, h=2)

        def direct_copies(unit):
            grp = wgrp.tile([P, 2, HALF, 4], BF16, name="grp", align_bytes=64)
            grp_tiles[unit] = grp
            for a in range(2):
                v_cols = VECTOR_COLS[a] if unit < VECTOR_UNITS else 0
                n_pe = pe_cols(unit, a)
                s_end = HALF - v_cols
                src = unit_src(unit, a)
                if v_cols:
                    nc.vector.tensor_copy(out=by_lines(grp[:, a, s_end:, :]), in_=rows_by_lines(src[:, :, s_end:]))
                nc.scalar.copy(out=by_lines(grp[:, a, n_pe:s_end, :]), in_=rows_by_lines(src[:, :, n_pe:s_end]))

        def empty_pass_through(unit):
            k, gp = unit // 2, unit % 2
            c, n = groups[k]
            for a in range(2):
                copy = nc.vector.tensor_copy if a == 1 and unit >= HEAD_UNITS else nc.scalar.copy
                n_pe = pe_cols(unit, a)
                copy(out=grp_tiles[unit][:, a, :n_pe, :], in_=pt_tiles[(unit, a)][:, :n_pe, :])
            if n == 1 and c + 2 < N_CHUNKS:
                load_weights(c + 2, 2 * gp, 0, CHUNK)
                load_weights(c + 2, 2 * gp + 1, 0, CHUNK)

        def quantise(unit):
            k, gp = unit // 2, unit % 2
            if gp == 0:
                wc = wcode.tile([P, PASSES, HALF], U32, name="wc", align_bytes=64)
                ws = wcode.tile([P, PASSES, HALF], U8, name="ws", align_bytes=64)
                code_tiles[k] = (wc, ws)
            wc, ws = code_tiles[k]
            nc.vector.quantize_mx(
                out=wc[:, 2 * gp : 2 * gp + 2, :].rearrange("p g c -> p (g c)").bitcast(FP8X4),
                scales=ws[:, 2 * gp : 2 * gp + 2, :].rearrange("p g c -> p (g c)"),
                in_=grp_tiles[unit][:].rearrange("p a c t -> p (a c t)"),
            )

        def matmuls(pair):
            k, b = pair // B, pair % B
            wc, ws = code_tiles[k]
            for e in range(2):
                m = 2 * b + e
                acc = accp.tile([P, 512], F32, name="acc", tag="acc")
                acc_tiles[(pair, e)] = acc
                for g in range(PASSES):
                    nc.tensor.matmul_mx(
                        out=acc[:],
                        lhsT=xc[:, m, P * g : P * (g + 1)].bitcast(FP8X4),
                        lhsT_scale=xs[:, m, P * g : P * (g + 1)],
                        rhs=wc[:, g, :].bitcast(FP8X4),
                        rhs_scale=ws[:, g, :],
                        start=(g == 0),
                        stop=(g == PASSES - 1),
                    )

        def products(pair):
            uw = ep.tile([P, 2, 4, 2, HD], F32, name="uw")
            r_t = rp.tile([P, 4, 2, HD], F32, name="r_t")
            pair_tiles[pair] = (uw, r_t)
            for e in range(2):
                nc.vector.tensor_tensor(
                    out=uw[:, :, :, e, :],
                    in0=acc_tiles[(pair, e)][:]
                    .rearrange("p (h d) -> p h d", h=4)
                    .unsqueeze(1)
                    .to_broadcast([P, 2, 4, HD]),
                    in1=cs[:, e, :, :, :]
                    .rearrange("p f i z -> p f (i z)")
                    .unsqueeze(2)
                    .to_broadcast([P, 2, 4, HD]),
                    op=MULT,
                )

        def add_and_store(engine, pair, lo, hi):
            k, b = pair // B, pair % B
            c, n = groups[k]
            uw, r_t = pair_tiles[pair]
            engine.tensor_tensor(
                out=r_t[:, lo:hi, :, :].rearrange("p h e (i z) -> p (h e i) z", z=2),
                in0=uw[:, 0, lo:hi, :, :].rearrange("p h e (i z) -> p (h e i) z", z=2),
                in1=uw[:, 1, lo:hi, :, :].rearrange("p h e (i z) -> p (h e i) z", z=2)[:, :, ::-1],
                op=ADD,
            )
            h0 = ((c % 2) * CHUNK + HALF * n) // HD
            nc.sync.dma_start(
                out=outs[c // 2][b, h0 + lo : h0 + hi, :, :].rearrange("h (p e) d -> p h (e d)", e=2),
                in_=r_t[:, lo:hi, :, :].rearrange("p h e d -> p h (e d)"),
            )

        def rotate(pair):
            products(pair)
            if pair < n_pairs - 2:
                add_and_store(nc.gpsimd, pair, 0, 4)
            elif pair == n_pairs - 2:
                add_and_store(nc.gpsimd, pair, 0, 2)
            else:
                add_and_store(nc.vector, pair - 1, 2, 4)
                for lo in (0, 2):
                    add_and_store(nc.vector, pair, lo, lo + 2)

        with tc.manual_schedule():
            load_x(0)
            load_x(1)
            for c in range(CHUNKS_IN_HALVES):
                for lo in (0, HALF):
                    for g in range(PASSES):
                        load_weights(c, g, lo, lo + HALF)
            for b in range(B):
                for e in range(2):
                    x_transposes(b, e)
                for e in range(2):
                    x_copies(b, e)
                for e in range(2):
                    x_quantise(b, e)
            pass_through(0)
            for step in range(n_units + LAG):
                pair = step - LAG
                if step < n_units:
                    direct_copies(step)
                    empty_pass_through(step)
                if step + 1 < n_units:
                    pass_through(step + 1)
                if step == 2:
                    matmuls(1)
                if 2 <= pair + 1 < n_pairs:
                    matmuls(pair + 1)
                if pair >= 0:
                    rotate(pair)
                if step < n_units:
                    quantise(step)
                if step == 1:
                    matmuls(0)
